import numpy as np
import ml_dtypes


def mxq(x, axis, fmt="e4m3"):
    dtype, down = {"e4m3": (ml_dtypes.float8_e4m3fn, 7), "e5m2": (ml_dtypes.float8_e5m2, 14)}[fmt]
    v = np.moveaxis(np.asarray(x, np.float32).astype(ml_dtypes.bfloat16).astype(np.float64), axis, -1)
    blocks = v.reshape(v.shape[:-1] + (-1, 32))
    amax = np.abs(blocks).max(-1, keepdims=True)
    byte = np.maximum(np.where(amax > 0, np.frexp(amax)[1] - 1 + 127, 0) - down, 1)
    scale = np.exp2(byte - 127.0)
    codes = (blocks / scale).astype(np.float32).astype(dtype).astype(np.float64)
    return np.moveaxis((codes * scale).reshape(v.shape), -1, axis)


WIDE = False


def mx_kscale(k):
    if not WIDE:
        return np.ones(k)
    levels = np.array([10, -10, 5, -5, 0])
    if k % 512:
        return np.exp2(np.random.permutation(np.resize(levels, k // 32))).repeat(32)
    a = np.empty((k // 512, 16))
    for p in range(k // 512):
        a[p, :8] = np.random.permutation(np.resize(levels, 8))
        for g in range(8):
            far = levels[np.abs(levels - a[p, g]) >= 10]
            a[p, g + 8] = far[np.random.randint(len(far))]
    return np.exp2(a.ravel()).repeat(32)


BF16 = ml_dtypes.bfloat16


def bf(x):
    return np.asarray(x, np.float32).astype(BF16)


def f64(x):
    return np.asarray(x).astype(np.float64)


B, I, H = 128, 512, 512
EPS = 1e-12
FORGET_BIAS = 1.0


def layer_norm(x, g, b):
    mean = np.mean(x, axis=-1, keepdims=True)
    var = np.mean((x - mean) ** 2, axis=-1, keepdims=True)
    var_filter = 0.01 * (var < EPS).astype(np.float64)
    normalized = (x - mean) / np.sqrt(var + EPS + var_filter)
    return g * normalized + b


def sigmoid(v):
    return 1.0 / (1.0 + np.exp(-v))


def setup_inputs():
    s, t = mx_kscale(I), mx_kscale(H)
    return {"x": bf(np.random.standard_normal((B, I)) * s),
            "hx": bf(np.random.standard_normal((B, H)) * t),
            "cx": bf(np.random.standard_normal((B, H))),
            "weight_ih": bf(np.random.standard_normal((4 * H, I)) / np.sqrt(I) / s[None, :]),
            "weight_hh": bf(np.random.standard_normal((4 * H, H)) / np.sqrt(H) / t[None, :]),
            "gamma": bf(1.0 + 0.1 * np.random.standard_normal((5, H))),
            "beta": bf(0.1 * np.random.standard_normal((5, H)))}


def reference(x, hx, cx, weight_ih, weight_hh, gamma, beta):
    cx, gamma, beta = f64(cx), f64(gamma), f64(beta)
    gates = (mxq(f64(x), 1, "e4m3") @ mxq(f64(weight_ih), 1, "e4m3").T) + (mxq(f64(hx), 1, "e4m3") @ mxq(f64(weight_hh), 1, "e4m3").T)
    ingate, forgetgate, cellgate, outgate = np.split(gates, 4, axis=1)
    ingate = layer_norm(ingate, gamma[0], beta[0])
    forgetgate = layer_norm(forgetgate, gamma[1], beta[1])
    cellgate = layer_norm(cellgate, gamma[2], beta[2])
    outgate = layer_norm(outgate, gamma[3], beta[3])
    ingate = sigmoid(ingate)
    forgetgate = sigmoid(forgetgate + FORGET_BIAS)
    cellgate = np.tanh(cellgate)
    outgate = sigmoid(outgate)
    cy = forgetgate * cx + ingate * cellgate
    cy = layer_norm(cy, gamma[4], beta[4])
    hy = outgate * np.tanh(cy)
    hy_dropped = hy
    return (hy_dropped, hy, cy)

@@ -1,0 +1,296 @@
+from contextlib import ExitStack
+
+import concourse.mybir as mybir
+from concourse.masks import make_identity
+
+F32 = mybir.dt.float32
+BF16 = mybir.dt.bfloat16
+I32 = mybir.dt.int32
+U32 = mybir.dt.uint32
+U8 = mybir.dt.uint8
+FP8X4 = mybir.dt.float8_e4m3fn_x4
+ALU = mybir.AluOpType
+ACT = mybir.ActivationFunctionType
+
+P = 128
+K = 512
+H = 512
+BANK = 512
+WORDS = K // 2
+ROW_BLOCKS = H // P
+GATES = 4
+I_GATE = 0
+F_GATE = 1
+G_GATE = 2
+O_GATE = 3
+CELL = GATES
+NORMS = GATES + 1
+EPS = 1e-12
+VAR_FLOOR = 0.01
+FORGET_BIAS = 1.0
+
+FLOPS = 2 * P * (GATES * H) * (2 * K)
+
+
+def tile_layernormdropoutlstmcell_s_kernel(
+    tc, x, hx, cx, weight_ih, weight_hh, gamma, beta, out_0, out_1, out_2
+):
+    nc = tc.nc
+    with ExitStack() as ctx:
+        ctx.enter_context(tc.manual_schedule())
+        consts = ctx.enter_context(tc.tile_pool(name="consts", bufs=1))
+        inputs = ctx.enter_context(tc.tile_pool(name="inputs", bufs=1))
+        staging = ctx.enter_context(tc.tile_pool(name="staging", bufs=4))
+        operands = ctx.enter_context(tc.tile_pool(name="operands", bufs=1))
+        kept = ctx.enter_context(tc.tile_pool(name="kept", bufs=1))
+        banks = ctx.enter_context(tc.psum_pool(name="banks", bufs=4))
+        sums = ctx.enter_context(tc.psum_pool(name="sums", bufs=4))
+
+        affine_rows = consts.tile([P, H], BF16)
+        nc.vector.memset(affine_rows[:].bitcast(I32), 0)
+        ident = consts.tile([P, P], F32)
+        make_identity(nc, ident[:])
+        minus_half = consts.tile([P, 1], F32)
+        nc.gpsimd.memset(minus_half[:], -0.5)
+        gate_bias = consts.tile([P, GATES], F32)
+        nc.gpsimd.memset(gate_bias[:], 0.0)
+        nc.gpsimd.memset(gate_bias[:, F_GATE : F_GATE + 1], FORGET_BIAS)
+        gate_func = (ACT.Sigmoid, ACT.Sigmoid, ACT.Tanh, ACT.Sigmoid)
+
+        table_warm = consts.tile([P, 1], F32)
+        nc.scalar.activation(out=table_warm[:], in_=minus_half[:], func=ACT.Sigmoid)
+
+        x_rows = inputs.tile([P, K], BF16)
+        nc.sync.dma_start(out=x_rows[:], in_=x[:, :])
+        nc.sync.dma_start(out=affine_rows[0:NORMS, :], in_=gamma[:, :])
+        nc.sync.dma_start(out=affine_rows[NORMS : 2 * NORMS, :], in_=beta[:, :])
+        hx_rows = inputs.tile([P, K], BF16)
+        nc.sync.dma_start(out=hx_rows[:], in_=hx[:, :])
+        cx_rows = inputs.tile([P, H], BF16)
+        w_rows = []
+        for g in range(GATES):
+            if g == O_GATE:
+                nc.sync.dma_start(out=cx_rows[:], in_=cx[:, :])
+            for weight in (weight_ih, weight_hh):
+                rows = inputs.tile([P, ROW_BLOCKS * K], BF16, name="w_rows_%d" % len(w_rows))
+                nc.sync.dma_start(
+                    out=rows[:].rearrange("p (b k) -> p b k", b=ROW_BLOCKS),
+                    in_=weight[g * H : (g + 1) * H, :].rearrange("(b p) k -> p b k", p=P),
+                )
+                w_rows.append(rows)
+
+        def new_bank():
+            bank = banks.tile([P, BANK], F32, name="bank")
+            return bank
+
+        def transpose_words(planes, column, rows_words):
+            for u in range(2):
+                nc.tensor.transpose(
+                    planes[:, u, column : column + P], rows_words[:, u : WORDS : 2], ident[:]
+                )
+
+        def regroup(grouped_words, planes):
+            nc.scalar.copy(
+                out=grouped_words.rearrange("p (c u) -> p c u", u=2),
+                in_=planes.rearrange("p u c -> p c u"),
+            )
+
+        spread_bank = {}
+        affine = {}
+
+        def spread_transposes(n):
+            spread_bank[n] = new_bank()
+            for s in range(2):
+                for u in range(2):
+                    column = (2 * s + u) * P
+                    row = s * NORMS + n
+                    nc.tensor.transpose(
+                        spread_bank[n][:, column : column + P],
+                        affine_cols[:, u, row : row + 1].to_broadcast([P, P]),
+                        ident[:],
+                    )
+
+        def spread_copy(n, copy):
+            affine[n] = consts.tile([P, 2 * H], BF16, name="affine_%d" % n)
+            copy(out=affine[n][:].bitcast(F32), in_=spread_bank[n][:])
+
+        grouped = {}
+        w_codes = {}
+        w_scales = {}
+
+        def unit_to_k_major(u):
+            grouped[u] = staging.tile([P, 4 * H], BF16, align_bytes=64, name="w_grouped")
+            grouped_words = grouped[u][:].bitcast(F32)
+            rows_words = w_rows[u][:].bitcast(F32)
+            for half in range(2):
+                bank = new_bank()
+                planes = bank[:].rearrange("p (u c) -> p u c", u=2)
+                for j in range(2):
+                    b = 2 * half + j
+                    transpose_words(planes, j * P, rows_words[:, b * WORDS : (b + 1) * WORDS])
+                regroup(grouped_words[:, half * BANK : (half + 1) * BANK], planes)
+
+        def quantise(u):
+            w_codes[u] = operands.tile([P, H], U32, align_bytes=64, name="w_codes_%d" % u)
+            w_scales[u] = operands.tile([P, H], U8, align_bytes=64, name="w_scales_%d" % u)
+            nc.vector.quantize_mx(
+                out=w_codes[u][:].bitcast(FP8X4), scales=w_scales[u][:], in_=grouped[u][:]
+            )
+
+        acc = {}
+
+        def mx_pass(u):
+            g, m = divmod(u, 2)
+            if m == 0:
+                acc[g] = sums.tile([P, H], F32, name="acc")
+            nc.tensor.matmul_mx(
+                out=acc[g][:],
+                lhsT=act_codes[:, m * P : (m + 1) * P].bitcast(FP8X4),
+                lhsT_scale=act_scales[:, m * P : (m + 1) * P],
+                rhs=w_codes[u][:].bitcast(FP8X4),
+                rhs_scale=w_scales[u][:],
+                start=(m == 0),
+                stop=(m == 1),
+            )
+
+        stats = {}
+        mean_var = {}
+        rstd = {}
+        centred = {}
+
+        def norm_stats(n, v):
+            stats[n] = kept.tile([P, 6], F32, name="stats_%d" % n)
+            nc.vector.bn_stats(out=stats[n][:], in_=v)
+
+        def norm_moments(n):
+            mean_var[n] = kept.tile([P, 2], F32, name="mean_var_%d" % n)
+            nc.vector.bn_aggr(out=mean_var[n][:], in_=stats[n][:])
+            var = mean_var[n][:, 1:2]
+            floor = kept.tile([P, 1], F32, name="floor_%d" % n)
+            nc.gpsimd.tensor_scalar(
+                out=floor[:], in0=var, scalar1=EPS, scalar2=VAR_FLOOR, op0=ALU.is_lt, op1=ALU.mult
+            )
+            padded = kept.tile([P, 1], F32, name="padded_%d" % n)
+            nc.gpsimd.tensor_scalar(
+                out=padded[:], in0=floor[:], scalar1=var, scalar2=EPS, op0=ALU.add, op1=ALU.add
+            )
+            rstd[n] = kept.tile([P, 1], F32, name="rstd_%d" % n)
+            nc.gpsimd.tensor_tensor(out=rstd[n][:], in0=padded[:], in1=minus_half[:], op=ALU.pow)
+
+        def norm_centre(n, v):
+            centred[n] = kept.tile([P, H], F32, name="centred_%d" % n)
+            nc.vector.scalar_tensor_tensor(
+                out=centred[n][:], in0=v, scalar=mean_var[n][:, 0:1], in1=affine[n][:, 0:H],
+                op0=ALU.subtract, op1=ALU.mult,
+            )
+
+        normed = {}
+
+        def norm_finish(n, cols):
+            if n not in normed:
+                normed[n] = kept.tile([P, H], F32, name="normed_%d" % n)
+            nc.vector.scalar_tensor_tensor(
+                out=normed[n][:, cols], in0=centred[n][:, cols], scalar=rstd[n][:],
+                in1=affine[n][:, H : 2 * H][:, cols], op0=ALU.mult, op1=ALU.add,
+            )
+
+        gate = {}
+
+        def apply_function(g):
+            gate[g] = kept.tile([P, H], F32, name="gate_%d" % g)
+            nc.scalar.activation(
+                out=gate[g][:], in_=normed[g][:], func=gate_func[g], bias=gate_bias[:, g : g + 1]
+            )
+
+        whole = slice(0, H)
+        halves = (slice(0, H // 2), slice(H // 2, H))
+
+        bank = new_bank()
+        planes = bank[:].rearrange("p (u c) -> p u c", u=2)
+        affine_words = affine_rows[:].bitcast(F32)
+        for u in range(2):
+            nc.tensor.transpose(planes[:, u, 0:P], affine_words[:, u * P : (u + 1) * P], ident[:])
+        affine_cols = consts.tile([P, 2, 2 * NORMS], F32)
+        nc.vector.tensor_copy(out=affine_cols[:], in_=planes[:, :, 0 : 2 * NORMS])
+
+        bank = new_bank()
+        planes = bank[:].rearrange("p (u c) -> p u c", u=2)
+        transpose_words(planes, 0, x_rows[:].bitcast(F32))
+        transpose_words(planes, P, hx_rows[:].bitcast(F32))
+        act_grouped = staging.tile([P, 4 * 2 * P], BF16, align_bytes=64)
+        regroup(act_grouped[:].bitcast(F32), planes)
+        act_codes = operands.tile([P, 2 * P], U32, align_bytes=64)
+        act_scales = operands.tile([P, 2 * P], U8, align_bytes=64)
+        nc.vector.quantize_mx(
+            out=act_codes[:].bitcast(FP8X4), scales=act_scales[:], in_=act_grouped[:]
+        )
+
+        for n in (I_GATE, F_GATE, G_GATE):
+            spread_transposes(n)
+        for n in (I_GATE, F_GATE, G_GATE):
+            spread_copy(n, nc.vector.tensor_copy)
+
+        for j in (I_GATE, F_GATE, G_GATE):
+            for u in (2 * j, 2 * j + 1):
+                unit_to_k_major(u)
+                if u >= 2:
+                    mx_pass(u - 2)
+            quantise(2 * j)
+            if j >= 1:
+                norm_stats(j - 1, acc[j - 1][:])
+            quantise(2 * j + 1)
+            if j >= 1:
+                norm_moments(j - 1)
+            if j >= 2:
+                norm_finish(j - 2, whole)
+            if j >= 1:
+                norm_centre(j - 1, acc[j - 1][:])
+
+        unit_to_k_major(2 * O_GATE)
+        mx_pass(2 * G_GATE)
+        mx_pass(2 * G_GATE + 1)
+        unit_to_k_major(2 * O_GATE + 1)
+        for n in (O_GATE, CELL):
+            spread_transposes(n)
+            spread_copy(n, nc.scalar.copy)
+
+        norm_stats(G_GATE, acc[G_GATE][:])
+        quantise(2 * O_GATE)
+        norm_moments(G_GATE)
+        quantise(2 * O_GATE + 1)
+        norm_centre(G_GATE, acc[G_GATE][:])
+        norm_finish(F_GATE, whole)
+        norm_finish(G_GATE, whole)
+        mx_pass(2 * O_GATE)
+        mx_pass(2 * O_GATE + 1)
+        for g in (I_GATE, F_GATE, G_GATE):
+            apply_function(g)
+
+        norm_stats(O_GATE, acc[O_GATE][:])
+        held = kept.tile([P, H], F32)
+        nc.vector.tensor_tensor(out=held[:], in0=gate[F_GATE][:], in1=cx_rows[:], op=ALU.mult)
+        fresh = kept.tile([P, H], F32)
+        nc.vector.tensor_tensor(out=fresh[:], in0=gate[I_GATE][:], in1=gate[G_GATE][:], op=ALU.mult)
+        norm_moments(O_GATE)
+        cell = kept.tile([P, H], F32)
+        nc.vector.tensor_tensor(out=cell[:], in0=held[:], in1=fresh[:], op=ALU.add)
+        norm_stats(CELL, cell[:])
+        norm_moments(CELL)
+        norm_centre(O_GATE, acc[O_GATE][:])
+        norm_centre(CELL, cell[:])
+        norm_finish(O_GATE, whole)
+        apply_function(O_GATE)
+
+        tanh_cy = kept.tile([P, H], F32)
+        hy = kept.tile([P, H], F32)
+        for cols in halves:
+            norm_finish(CELL, cols)
+        nc.sync.dma_start(out=out_2[:, :], in_=normed[CELL][:])
+        for cols in halves:
+            nc.scalar.activation(out=tanh_cy[:, cols], in_=normed[CELL][:, cols], func=ACT.Tanh)
+        for cols in halves:
+            nc.vector.tensor_tensor(
+                out=hy[:, cols], in0=gate[O_GATE][:, cols], in1=tanh_cy[:, cols], op=ALU.mult
+            )
+            nc.sync.dma_start(out=out_0[:, cols], in_=hy[:, cols])
+            nc.sync.dma_start(out=out_1[:, cols], in_=hy[:, cols])

@@ -5,7 +5,6 @@ from concourse.masks import make_identity
 
 F32 = mybir.dt.float32
 BF16 = mybir.dt.bfloat16
-I32 = mybir.dt.int32
 U32 = mybir.dt.uint32
 U8 = mybir.dt.uint8
 FP8X4 = mybir.dt.float8_e4m3fn_x4
@@ -18,12 +17,13 @@ H = 512
 BANK = 512
 WORDS = K // 2
 ROW_BLOCKS = H // P
-GATES = 4
 I_GATE = 0
 F_GATE = 1
 G_GATE = 2
 O_GATE = 3
-CELL = GATES
+CELL = 4
+ORDER = (F_GATE, I_GATE, G_GATE, O_GATE)
+GATES = len(ORDER)
 NORMS = GATES + 1
 EPS = 1e-12
 VAR_FLOOR = 0.01
@@ -46,10 +46,10 @@ def tile_layernormdropoutlstmcell_s_kernel(
         banks = ctx.enter_context(tc.psum_pool(name="banks", bufs=4))
         sums = ctx.enter_context(tc.psum_pool(name="sums", bufs=4))
 
-        affine_rows = consts.tile([P, H], BF16)
-        nc.vector.memset(affine_rows[:].bitcast(I32), 0)
         ident = consts.tile([P, P], F32)
         make_identity(nc, ident[:])
+        ident_bf16 = consts.tile([P, P], BF16)
+        nc.vector.tensor_copy(out=ident_bf16[:], in_=ident[:])
         minus_half = consts.tile([P, 1], F32)
         nc.gpsimd.memset(minus_half[:], -0.5)
         gate_bias = consts.tile([P, GATES], F32)
@@ -60,28 +60,64 @@ def tile_layernormdropoutlstmcell_s_kernel(
         table_warm = consts.tile([P, 1], F32)
         nc.scalar.activation(out=table_warm[:], in_=minus_half[:], func=ACT.Sigmoid)
 
+        o_affine_rows = inputs.tile([P, H], BF16)
+        nc.vector.memset(o_affine_rows[:], 0.0)
         x_rows = inputs.tile([P, K], BF16)
-        nc.sync.dma_start(out=x_rows[:], in_=x[:, :])
-        nc.sync.dma_start(out=affine_rows[0:NORMS, :], in_=gamma[:, :])
-        nc.sync.dma_start(out=affine_rows[NORMS : 2 * NORMS, :], in_=beta[:, :])
         hx_rows = inputs.tile([P, K], BF16)
-        nc.sync.dma_start(out=hx_rows[:], in_=hx[:, :])
         cx_rows = inputs.tile([P, H], BF16)
         w_rows = []
-        for g in range(GATES):
-            if g == O_GATE:
-                nc.sync.dma_start(out=cx_rows[:], in_=cx[:, :])
-            for weight in (weight_ih, weight_hh):
-                rows = inputs.tile([P, ROW_BLOCKS * K], BF16, name="w_rows_%d" % len(w_rows))
+
+        def load_unit(parts):
+            u = len(w_rows)
+            gate, weight = ORDER[u // 2], (weight_ih, weight_hh)[u % 2]
+            blocks = ROW_BLOCKS // parts
+            tiles = []
+            for part in range(parts):
+                rows = inputs.tile([P, blocks * K], BF16, name="w_rows_%d_%d" % (u, part))
+                first = gate * H + part * blocks * P
                 nc.sync.dma_start(
-                    out=rows[:].rearrange("p (b k) -> p b k", b=ROW_BLOCKS),
-                    in_=weight[g * H : (g + 1) * H, :].rearrange("(b p) k -> p b k", p=P),
+                    out=rows[:].rearrange("p (b k) -> p b k", b=blocks),
+                    in_=weight[first : first + blocks * P, :].rearrange("(b p) k -> p b k", p=P),
                 )
-                w_rows.append(rows)
+                tiles.append(rows)
+            w_rows.append((tiles, blocks))
+
+        affine = {}
+
+        def load_affine(first, count):
+            rows = slice(first, first + count)
+            for name, source in (("gamma", gamma), ("beta", beta)):
+                spread = consts.tile([P, count * H], BF16, name="%s_%d" % (name, first))
+                nc.sync.dma_start(
+                    out=spread[:],
+                    in_=source[rows, :].rearrange("n h -> (n h)").partition_broadcast(P),
+                )
+                for n in range(count):
+                    affine[name, first + n] = spread[:, n * H : (n + 1) * H]
+
+        load_unit(4)
+        load_unit(2)
+        nc.sync.dma_start(out=x_rows[:], in_=x[:, :])
+        nc.sync.dma_start(out=hx_rows[:], in_=hx[:, :])
+        load_unit(1)
+        load_unit(1)
+        load_affine(I_GATE, 2)
+        load_unit(1)
+        load_unit(1)
+        nc.sync.dma_start(out=cx_rows[:], in_=cx[:, :])
+        load_unit(1)
+        load_affine(G_GATE, 1)
+        load_unit(1)
+        nc.sync.dma_start(out=o_affine_rows[0:1, :], in_=gamma[O_GATE : O_GATE + 1, :])
+        nc.sync.dma_start(out=o_affine_rows[1:2, :], in_=beta[O_GATE : O_GATE + 1, :])
+        load_affine(CELL, 1)
 
         def new_bank():
             bank = banks.tile([P, BANK], F32, name="bank")
-            return bank
+            return bank[:]
+
+        def new_planes():
+            return new_bank().rearrange("p (u c) -> p u c", u=2)
 
         def transpose_words(planes, column, rows_words):
             for u in range(2):
@@ -89,30 +125,11 @@ def tile_layernormdropoutlstmcell_s_kernel(
                     planes[:, u, column : column + P], rows_words[:, u : WORDS : 2], ident[:]
                 )
 
-        def regroup(grouped_words, planes):
-            nc.scalar.copy(
+        def regroup(copy, grouped_words, planes):
+            copy(
                 out=grouped_words.rearrange("p (c u) -> p c u", u=2),
                 in_=planes.rearrange("p u c -> p c u"),
             )
-
-        spread_bank = {}
-        affine = {}
-
-        def spread_transposes(n):
-            spread_bank[n] = new_bank()
-            for s in range(2):
-                for u in range(2):
-                    column = (2 * s + u) * P
-                    row = s * NORMS + n
-                    nc.tensor.transpose(
-                        spread_bank[n][:, column : column + P],
-                        affine_cols[:, u, row : row + 1].to_broadcast([P, P]),
-                        ident[:],
-                    )
-
-        def spread_copy(n, copy):
-            affine[n] = consts.tile([P, 2 * H], BF16, name="affine_%d" % n)
-            copy(out=affine[n][:].bitcast(F32), in_=spread_bank[n][:])
 
         grouped = {}
         w_codes = {}
@@ -121,26 +138,30 @@ def tile_layernormdropoutlstmcell_s_kernel(
         def unit_to_k_major(u):
             grouped[u] = staging.tile([P, 4 * H], BF16, align_bytes=64, name="w_grouped")
             grouped_words = grouped[u][:].bitcast(F32)
-            rows_words = w_rows[u][:].bitcast(F32)
+            tiles, blocks = w_rows[u]
             for half in range(2):
-                bank = new_bank()
-                planes = bank[:].rearrange("p (u c) -> p u c", u=2)
+                planes = new_planes()
                 for j in range(2):
-                    b = 2 * half + j
+                    part, b = divmod(2 * half + j, blocks)
+                    rows_words = tiles[part][:].bitcast(F32)
                     transpose_words(planes, j * P, rows_words[:, b * WORDS : (b + 1) * WORDS])
-                regroup(grouped_words[:, half * BANK : (half + 1) * BANK], planes)
+                regroup(nc.scalar.copy, grouped_words[:, half * BANK : (half + 1) * BANK], planes)
 
-        def quantise(u):
+        def quantise(u, parts=1):
             w_codes[u] = operands.tile([P, H], U32, align_bytes=64, name="w_codes_%d" % u)
             w_scales[u] = operands.tile([P, H], U8, align_bytes=64, name="w_scales_%d" % u)
-            nc.vector.quantize_mx(
-                out=w_codes[u][:].bitcast(FP8X4), scales=w_scales[u][:], in_=grouped[u][:]
-            )
+            width = H // parts
+            for part in range(parts):
+                cols = slice(part * width, (part + 1) * width)
+                nc.vector.quantize_mx(
+                    out=w_codes[u][:, cols].bitcast(FP8X4), scales=w_scales[u][:, cols],
+                    in_=grouped[u][:, 4 * part * width : 4 * (part + 1) * width],
+                )
 
         acc = {}
 
         def mx_pass(u):
-            g, m = divmod(u, 2)
+            g, m = ORDER[u // 2], u % 2
             if m == 0:
                 acc[g] = sums.tile([P, H], F32, name="acc")
             nc.tensor.matmul_mx(
@@ -167,11 +188,11 @@ def tile_layernormdropoutlstmcell_s_kernel(
             nc.vector.bn_aggr(out=mean_var[n][:], in_=stats[n][:])
             var = mean_var[n][:, 1:2]
             floor = kept.tile([P, 1], F32, name="floor_%d" % n)
-            nc.gpsimd.tensor_scalar(
+            nc.vector.tensor_scalar(
                 out=floor[:], in0=var, scalar1=EPS, scalar2=VAR_FLOOR, op0=ALU.is_lt, op1=ALU.mult
             )
             padded = kept.tile([P, 1], F32, name="padded_%d" % n)
-            nc.gpsimd.tensor_scalar(
+            nc.vector.tensor_scalar(
                 out=padded[:], in0=floor[:], scalar1=var, scalar2=EPS, op0=ALU.add, op1=ALU.add
             )
             rstd[n] = kept.tile([P, 1], F32, name="rstd_%d" % n)
@@ -180,7 +201,7 @@ def tile_layernormdropoutlstmcell_s_kernel(
         def norm_centre(n, v):
             centred[n] = kept.tile([P, H], F32, name="centred_%d" % n)
             nc.vector.scalar_tensor_tensor(
-                out=centred[n][:], in0=v, scalar=mean_var[n][:, 0:1], in1=affine[n][:, 0:H],
+                out=centred[n][:], in0=v, scalar=mean_var[n][:, 0:1], in1=affine["gamma", n],
                 op0=ALU.subtract, op1=ALU.mult,
             )
 
@@ -191,95 +212,122 @@ def tile_layernormdropoutlstmcell_s_kernel(
                 normed[n] = kept.tile([P, H], F32, name="normed_%d" % n)
             nc.vector.scalar_tensor_tensor(
                 out=normed[n][:, cols], in0=centred[n][:, cols], scalar=rstd[n][:],
-                in1=affine[n][:, H : 2 * H][:, cols], op0=ALU.mult, op1=ALU.add,
+                in1=affine["beta", n][:, cols], op0=ALU.mult, op1=ALU.add,
             )
 
         gate = {}
 
-        def apply_function(g):
-            gate[g] = kept.tile([P, H], F32, name="gate_%d" % g)
+        def apply_function(g, cols):
+            if g not in gate:
+                gate[g] = kept.tile([P, H], F32, name="gate_%d" % g)
             nc.scalar.activation(
-                out=gate[g][:], in_=normed[g][:], func=gate_func[g], bias=gate_bias[:, g : g + 1]
+                out=gate[g][:, cols], in_=normed[g][:, cols], func=gate_func[g],
+                bias=gate_bias[:, g : g + 1],
             )
 
         whole = slice(0, H)
         halves = (slice(0, H // 2), slice(H // 2, H))
 
-        bank = new_bank()
-        planes = bank[:].rearrange("p (u c) -> p u c", u=2)
-        affine_words = affine_rows[:].bitcast(F32)
-        for u in range(2):
-            nc.tensor.transpose(planes[:, u, 0:P], affine_words[:, u * P : (u + 1) * P], ident[:])
-        affine_cols = consts.tile([P, 2, 2 * NORMS], F32)
-        nc.vector.tensor_copy(out=affine_cols[:], in_=planes[:, :, 0 : 2 * NORMS])
-
-        bank = new_bank()
-        planes = bank[:].rearrange("p (u c) -> p u c", u=2)
+        unit_to_k_major(0)
+        unit_to_k_major(1)
+        planes = new_planes()
         transpose_words(planes, 0, x_rows[:].bitcast(F32))
         transpose_words(planes, P, hx_rows[:].bitcast(F32))
         act_grouped = staging.tile([P, 4 * 2 * P], BF16, align_bytes=64)
-        regroup(act_grouped[:].bitcast(F32), planes)
+        quantise(0)
+        regroup(nc.vector.tensor_copy, act_grouped[:].bitcast(F32), planes)
         act_codes = operands.tile([P, 2 * P], U32, align_bytes=64)
         act_scales = operands.tile([P, 2 * P], U8, align_bytes=64)
         nc.vector.quantize_mx(
             out=act_codes[:].bitcast(FP8X4), scales=act_scales[:], in_=act_grouped[:]
         )
-
-        for n in (I_GATE, F_GATE, G_GATE):
-            spread_transposes(n)
-        for n in (I_GATE, F_GATE, G_GATE):
-            spread_copy(n, nc.vector.tensor_copy)
-
-        for j in (I_GATE, F_GATE, G_GATE):
-            for u in (2 * j, 2 * j + 1):
-                unit_to_k_major(u)
-                if u >= 2:
-                    mx_pass(u - 2)
-            quantise(2 * j)
-            if j >= 1:
-                norm_stats(j - 1, acc[j - 1][:])
-            quantise(2 * j + 1)
-            if j >= 1:
-                norm_moments(j - 1)
-            if j >= 2:
-                norm_finish(j - 2, whole)
-            if j >= 1:
-                norm_centre(j - 1, acc[j - 1][:])
-
-        unit_to_k_major(2 * O_GATE)
-        mx_pass(2 * G_GATE)
-        mx_pass(2 * G_GATE + 1)
-        unit_to_k_major(2 * O_GATE + 1)
-        for n in (O_GATE, CELL):
-            spread_transposes(n)
-            spread_copy(n, nc.scalar.copy)
-
-        norm_stats(G_GATE, acc[G_GATE][:])
-        quantise(2 * O_GATE)
-        norm_moments(G_GATE)
-        quantise(2 * O_GATE + 1)
-        norm_centre(G_GATE, acc[G_GATE][:])
+        quantise(1)
+        unit_to_k_major(2)
+        mx_pass(0)
+        mx_pass(1)
+        quantise(2)
+        norm_stats(F_GATE, acc[F_GATE][:])
+        norm_moments(F_GATE)
+        norm_centre(F_GATE, acc[F_GATE][:])
+        unit_to_k_major(3)
+        quantise(3)
         norm_finish(F_GATE, whole)
-        norm_finish(G_GATE, whole)
-        mx_pass(2 * O_GATE)
-        mx_pass(2 * O_GATE + 1)
-        for g in (I_GATE, F_GATE, G_GATE):
-            apply_function(g)
+        unit_to_k_major(4)
+        mx_pass(2)
+        mx_pass(3)
+        quantise(4)
+        norm_stats(I_GATE, acc[I_GATE][:])
+        norm_moments(I_GATE)
+        norm_centre(I_GATE, acc[I_GATE][:])
+        unit_to_k_major(5)
+        apply_function(F_GATE, whole)
+        unit_to_k_major(6)
+        quantise(5, 2)
+        mx_pass(4)
+        mx_pass(5)
+        norm_finish(I_GATE, whole)
+        held = kept.tile([P, H], F32)
+        nc.gpsimd.tensor_tensor(out=held[:], in0=gate[F_GATE][:], in1=cx_rows[:], op=ALU.mult)
+
+        unit_to_k_major(7)
+        norm_stats(G_GATE, acc[G_GATE][:])
+        norm_moments(G_GATE)
+        norm_centre(G_GATE, acc[G_GATE][:])
+        quantise(6)
+        o_affine_bank = new_bank().bitcast(BF16)[:, 0:H]
+        for j in range(H // P):
+            block = slice(j * P, (j + 1) * P)
+            nc.tensor.transpose(o_affine_bank[:, block], o_affine_rows[:, block], ident_bf16[:])
+        o_affine = consts.tile([P, 2, H // P], F32)
+        nc.vector.tensor_copy(
+            out=o_affine[:],
+            in_=o_affine_bank.rearrange("p (j r) -> p r j", r=P)[:, 0:2, :],
+        )
+
+        mx_pass(6)
+        apply_function(I_GATE, whole)
+        quantise(7)
+        mx_pass(7)
+        for cols in halves:
+            norm_finish(G_GATE, cols)
+        for cols in halves:
+            apply_function(G_GATE, cols)
 
         norm_stats(O_GATE, acc[O_GATE][:])
-        held = kept.tile([P, H], F32)
-        nc.vector.tensor_tensor(out=held[:], in0=gate[F_GATE][:], in1=cx_rows[:], op=ALU.mult)
+        norm_moments(O_GATE)
+        o_shift = kept.tile([P, 1], F32)
+        nc.gpsimd.tensor_scalar(
+            out=o_shift[:], in0=mean_var[O_GATE][:, 0:1], scalar1=rstd[O_GATE][:], scalar2=-1.0,
+            op0=ALU.mult, op1=ALU.mult,
+        )
         fresh = kept.tile([P, H], F32)
         nc.vector.tensor_tensor(out=fresh[:], in0=gate[I_GATE][:], in1=gate[G_GATE][:], op=ALU.mult)
-        norm_moments(O_GATE)
         cell = kept.tile([P, H], F32)
         nc.vector.tensor_tensor(out=cell[:], in0=held[:], in1=fresh[:], op=ALU.add)
         norm_stats(CELL, cell[:])
         norm_moments(CELL)
-        norm_centre(O_GATE, acc[O_GATE][:])
         norm_centre(CELL, cell[:])
-        norm_finish(O_GATE, whole)
-        apply_function(O_GATE)
+
+        o_unit = kept.tile([P, H], F32)
+        nc.scalar.activation(
+            out=o_unit[:], in_=acc[O_GATE][:], func=ACT.Identity,
+            bias=o_shift[:], scale=rstd[O_GATE][:],
+        )
+        o_turned_bank = new_bank()
+        o_turned = kept.tile([P, H], F32)
+        o_bank = new_bank()
+        for j in range(H // P):
+            block = slice(j * P, (j + 1) * P)
+            nc.tensor.transpose(o_turned_bank[:, block], o_unit[:, block], ident[:])
+        for j in range(H // P):
+            block = slice(j * P, (j + 1) * P)
+            nc.scalar.activation(
+                out=o_turned[:, block], in_=o_turned_bank[:, block], func=ACT.Sigmoid,
+                bias=o_affine[:, 1, j : j + 1], scale=o_affine[:, 0, j : j + 1],
+            )
+        for j in range(H // P):
+            block = slice(j * P, (j + 1) * P)
+            nc.tensor.transpose(o_bank[:, block], o_turned[:, block], ident[:])
 
         tanh_cy = kept.tile([P, H], F32)
         hy = kept.tile([P, H], F32)
@@ -290,7 +338,7 @@ def tile_layernormdropoutlstmcell_s_kernel(
             nc.scalar.activation(out=tanh_cy[:, cols], in_=normed[CELL][:, cols], func=ACT.Tanh)
         for cols in halves:
             nc.vector.tensor_tensor(
-                out=hy[:, cols], in0=gate[O_GATE][:, cols], in1=tanh_cy[:, cols], op=ALU.mult
+                out=hy[:, cols], in0=o_bank[:, cols], in1=tanh_cy[:, cols], op=ALU.mult
             )
             nc.sync.dma_start(out=out_0[:, cols], in_=hy[:, cols])
             nc.sync.dma_start(out=out_1[:, cols], in_=hy[:, cols])

@@ -43,9 +43,11 @@ def tile_layernormdropoutlstmcell_s_kernel(
         staging = ctx.enter_context(tc.tile_pool(name="staging", bufs=4))
         operands = ctx.enter_context(tc.tile_pool(name="operands", bufs=1))
         kept = ctx.enter_context(tc.tile_pool(name="kept", bufs=1))
-        banks = ctx.enter_context(tc.psum_pool(name="banks", bufs=4))
-        sums = ctx.enter_context(tc.psum_pool(name="sums", bufs=4))
+        banks = ctx.enter_context(tc.psum_pool(name="banks", bufs=6))
+        sums = ctx.enter_context(tc.psum_pool(name="sums", bufs=2))
 
+        affine_rows = inputs.tile([P, H], BF16)
+        nc.vector.memset(affine_rows[:], 0.0)
         ident = consts.tile([P, P], F32)
         make_identity(nc, ident[:])
         ident_bf16 = consts.tile([P, P], BF16)
@@ -57,11 +59,6 @@ def tile_layernormdropoutlstmcell_s_kernel(
         nc.gpsimd.memset(gate_bias[:, F_GATE : F_GATE + 1], FORGET_BIAS)
         gate_func = (ACT.Sigmoid, ACT.Sigmoid, ACT.Tanh, ACT.Sigmoid)
 
-        table_warm = consts.tile([P, 1], F32)
-        nc.scalar.activation(out=table_warm[:], in_=minus_half[:], func=ACT.Sigmoid)
-
-        o_affine_rows = inputs.tile([P, H], BF16)
-        nc.vector.memset(o_affine_rows[:], 0.0)
         x_rows = inputs.tile([P, K], BF16)
         hx_rows = inputs.tile([P, K], BF16)
         cx_rows = inputs.tile([P, H], BF16)
@@ -82,35 +79,29 @@ def tile_layernormdropoutlstmcell_s_kernel(
                 tiles.append(rows)
             w_rows.append((tiles, blocks))
 
-        affine = {}
+        gamma_row = (0, 1, 2, 3, 8)
+        beta_row = (4, 5, 6, 7, 9)
+        for first, last, row in ((0, GATES, 0), (CELL, NORMS, 2 * GATES)):
+            count = last - first
+            nc.scalar.dma_start(out=affine_rows[row : row + count, :], in_=gamma[first:last, :])
+            nc.scalar.dma_start(
+                out=affine_rows[row + count : row + 2 * count, :], in_=beta[first:last, :]
+            )
 
-        def load_affine(first, count):
-            rows = slice(first, first + count)
-            for name, source in (("gamma", gamma), ("beta", beta)):
-                spread = consts.tile([P, count * H], BF16, name="%s_%d" % (name, first))
-                nc.sync.dma_start(
-                    out=spread[:],
-                    in_=source[rows, :].rearrange("n h -> (n h)").partition_broadcast(P),
-                )
-                for n in range(count):
-                    affine[name, first + n] = spread[:, n * H : (n + 1) * H]
+        table_warm = consts.tile([P, 1], F32)
+        nc.scalar.activation(out=table_warm[:], in_=minus_half[:], func=ACT.Sigmoid)
 
-        load_unit(4)
         load_unit(2)
+        load_unit(1)
         nc.sync.dma_start(out=x_rows[:], in_=x[:, :])
         nc.sync.dma_start(out=hx_rows[:], in_=hx[:, :])
         load_unit(1)
         load_unit(1)
-        load_affine(I_GATE, 2)
         load_unit(1)
         load_unit(1)
         nc.sync.dma_start(out=cx_rows[:], in_=cx[:, :])
         load_unit(1)
-        load_affine(G_GATE, 1)
         load_unit(1)
-        nc.sync.dma_start(out=o_affine_rows[0:1, :], in_=gamma[O_GATE : O_GATE + 1, :])
-        nc.sync.dma_start(out=o_affine_rows[1:2, :], in_=beta[O_GATE : O_GATE + 1, :])
-        load_affine(CELL, 1)
 
         def new_bank():
             bank = banks.tile([P, BANK], F32, name="bank")
@@ -130,6 +121,27 @@ def tile_layernormdropoutlstmcell_s_kernel(
                 out=grouped_words.rearrange("p (c u) -> p c u", u=2),
                 in_=planes.rearrange("p u c -> p c u"),
             )
+
+        affine = {}
+
+        spread_bank = {}
+
+        def spread_transposes(n):
+            spread_bank[n] = new_bank()
+            for s, row in enumerate((gamma_row[n], beta_row[n])):
+                for u in range(2):
+                    column = (2 * s + u) * P
+                    nc.tensor.transpose(
+                        spread_bank[n][:, column : column + P],
+                        affine_cols[:, u, row : row + 1].to_broadcast([P, P]),
+                        ident[:],
+                    )
+
+        def spread_copy(n, copy):
+            spread = consts.tile([P, 2 * H], BF16, name="affine_%d" % n)
+            copy(out=spread[:].bitcast(F32), in_=spread_bank[n])
+            affine["gamma", n] = spread[:, 0:H]
+            affine["beta", n] = spread[:, H : 2 * H]
 
         grouped = {}
         w_codes = {}
@@ -160,49 +172,63 @@ def tile_layernormdropoutlstmcell_s_kernel(
 
         acc = {}
 
-        def mx_pass(u):
-            g, m = ORDER[u // 2], u % 2
-            if m == 0:
-                acc[g] = sums.tile([P, H], F32, name="acc")
-            nc.tensor.matmul_mx(
-                out=acc[g][:],
-                lhsT=act_codes[:, m * P : (m + 1) * P].bitcast(FP8X4),
-                lhsT_scale=act_scales[:, m * P : (m + 1) * P],
-                rhs=w_codes[u][:].bitcast(FP8X4),
-                rhs_scale=w_scales[u][:],
-                start=(m == 0),
-                stop=(m == 1),
-            )
+        def mx_gate(g, parts=1):
+            acc[g] = sums.tile([P, H], F32, name="acc")
+            width = H // parts
+            for part in range(parts):
+                cols = slice(part * width, (part + 1) * width)
+                for m in range(2):
+                    u = 2 * ORDER.index(g) + m
+                    nc.tensor.matmul_mx(
+                        out=acc[g][:, cols],
+                        lhsT=act_codes[:, m * P : (m + 1) * P].bitcast(FP8X4),
+                        lhsT_scale=act_scales[:, m * P : (m + 1) * P],
+                        rhs=w_codes[u][:, cols].bitcast(FP8X4),
+                        rhs_scale=w_scales[u][:, cols],
+                        start=(m == 0),
+                        stop=(m == 1),
+                    )
 
+        whole = slice(0, H)
+        halves = (slice(0, H // 2), slice(H // 2, H))
         stats = {}
         mean_var = {}
         rstd = {}
         centred = {}
 
-        def norm_stats(n, v):
-            stats[n] = kept.tile([P, 6], F32, name="stats_%d" % n)
-            nc.vector.bn_stats(out=stats[n][:], in_=v)
+        def norm_stats(n, v, parts):
+            stats[n] = kept.tile([P, len(parts), 6], F32, name="stats_%d" % n)
+            for part, cols in enumerate(parts):
+                nc.vector.bn_stats(out=stats[n][:, part, :], in_=v[:, cols])
 
-        def norm_moments(n):
+        def norm_mean(n):
             mean_var[n] = kept.tile([P, 2], F32, name="mean_var_%d" % n)
-            nc.vector.bn_aggr(out=mean_var[n][:], in_=stats[n][:])
-            var = mean_var[n][:, 1:2]
-            floor = kept.tile([P, 1], F32, name="floor_%d" % n)
-            nc.vector.tensor_scalar(
-                out=floor[:], in0=var, scalar1=EPS, scalar2=VAR_FLOOR, op0=ALU.is_lt, op1=ALU.mult
+            nc.vector.bn_aggr(out=mean_var[n][:], in_=stats[n][:].rearrange("p s k -> p (s k)"))
+
+        floor = {}
+
+        def norm_floor(n, engine):
+            floor[n] = kept.tile([P, 1], F32, name="floor_%d" % n)
+            engine.tensor_scalar(
+                out=floor[n][:], in0=mean_var[n][:, 1:2], scalar1=EPS, scalar2=VAR_FLOOR,
+                op0=ALU.is_lt, op1=ALU.mult,
             )
+
+        def norm_rstd(n, engine):
             padded = kept.tile([P, 1], F32, name="padded_%d" % n)
-            nc.vector.tensor_scalar(
-                out=padded[:], in0=floor[:], scalar1=var, scalar2=EPS, op0=ALU.add, op1=ALU.add
+            engine.tensor_scalar(
+                out=padded[:], in0=floor[n][:], scalar1=mean_var[n][:, 1:2], scalar2=EPS,
+                op0=ALU.add, op1=ALU.add,
             )
             rstd[n] = kept.tile([P, 1], F32, name="rstd_%d" % n)
             nc.gpsimd.tensor_tensor(out=rstd[n][:], in0=padded[:], in1=minus_half[:], op=ALU.pow)
 
-        def norm_centre(n, v):
-            centred[n] = kept.tile([P, H], F32, name="centred_%d" % n)
+        def norm_centre(n, v, cols):
+            if n not in centred:
+                centred[n] = kept.tile([P, H], F32, name="centred_%d" % n)
             nc.vector.scalar_tensor_tensor(
-                out=centred[n][:], in0=v, scalar=mean_var[n][:, 0:1], in1=affine["gamma", n],
-                op0=ALU.subtract, op1=ALU.mult,
+                out=centred[n][:, cols], in0=v[:, cols], scalar=mean_var[n][:, 0:1],
+                in1=affine["gamma", n][:, cols], op0=ALU.subtract, op1=ALU.mult,
             )
 
         normed = {}
@@ -225,94 +251,124 @@ def tile_layernormdropoutlstmcell_s_kernel(
                 bias=gate_bias[:, g : g + 1],
             )
 
-        whole = slice(0, H)
-        halves = (slice(0, H // 2), slice(H // 2, H))
-
+        planes = new_planes()
+        affine_words = affine_rows[:].bitcast(F32)
+        for u in range(2):
+            nc.tensor.transpose(planes[:, u, 0:P], affine_words[:, u * P : (u + 1) * P], ident[:])
+        affine_cols = consts.tile([P, 2, 2 * NORMS], F32)
+        nc.vector.tensor_copy(out=affine_cols[:], in_=planes[:, :, 0 : 2 * NORMS])
         unit_to_k_major(0)
+        spread_transposes(F_GATE)
         unit_to_k_major(1)
+        quantise(0)
+        spread_copy(F_GATE, nc.vector.tensor_copy)
         planes = new_planes()
         transpose_words(planes, 0, x_rows[:].bitcast(F32))
         transpose_words(planes, P, hx_rows[:].bitcast(F32))
         act_grouped = staging.tile([P, 4 * 2 * P], BF16, align_bytes=64)
-        quantise(0)
         regroup(nc.vector.tensor_copy, act_grouped[:].bitcast(F32), planes)
         act_codes = operands.tile([P, 2 * P], U32, align_bytes=64)
         act_scales = operands.tile([P, 2 * P], U8, align_bytes=64)
+        quantise(1)
         nc.vector.quantize_mx(
             out=act_codes[:].bitcast(FP8X4), scales=act_scales[:], in_=act_grouped[:]
         )
-        quantise(1)
+        spread_transposes(I_GATE)
         unit_to_k_major(2)
-        mx_pass(0)
-        mx_pass(1)
+        mx_gate(F_GATE)
+        spread_copy(I_GATE, nc.vector.tensor_copy)
         quantise(2)
-        norm_stats(F_GATE, acc[F_GATE][:])
-        norm_moments(F_GATE)
-        norm_centre(F_GATE, acc[F_GATE][:])
+        norm_stats(F_GATE, acc[F_GATE], (whole,))
         unit_to_k_major(3)
+        norm_mean(F_GATE)
+        norm_floor(F_GATE, nc.gpsimd)
+        norm_rstd(F_GATE, nc.gpsimd)
         quantise(3)
-        norm_finish(F_GATE, whole)
+        norm_centre(F_GATE, acc[F_GATE], whole)
         unit_to_k_major(4)
-        mx_pass(2)
-        mx_pass(3)
+        mx_gate(I_GATE)
         quantise(4)
-        norm_stats(I_GATE, acc[I_GATE][:])
-        norm_moments(I_GATE)
-        norm_centre(I_GATE, acc[I_GATE][:])
+        norm_finish(F_GATE, whole)
+        norm_stats(I_GATE, acc[I_GATE], (whole,))
+        norm_mean(I_GATE)
+        norm_floor(I_GATE, nc.gpsimd)
+        norm_rstd(I_GATE, nc.gpsimd)
         unit_to_k_major(5)
+        spread_transposes(G_GATE)
+        quantise(5, 2)
+        mx_gate(G_GATE, 2)
+        spread_copy(G_GATE, nc.scalar.copy)
         apply_function(F_GATE, whole)
         unit_to_k_major(6)
-        quantise(5, 2)
-        mx_pass(4)
-        mx_pass(5)
-        norm_finish(I_GATE, whole)
+        norm_centre(I_GATE, acc[I_GATE], whole)
         held = kept.tile([P, H], F32)
         nc.gpsimd.tensor_tensor(out=held[:], in0=gate[F_GATE][:], in1=cx_rows[:], op=ALU.mult)
 
         unit_to_k_major(7)
-        norm_stats(G_GATE, acc[G_GATE][:])
-        norm_moments(G_GATE)
-        norm_centre(G_GATE, acc[G_GATE][:])
+        norm_stats(G_GATE, acc[G_GATE], halves)
+        norm_finish(I_GATE, whole)
+        norm_mean(G_GATE)
+        norm_floor(G_GATE, nc.vector)
+        norm_centre(G_GATE, acc[G_GATE], whole)
+        norm_rstd(G_GATE, nc.vector)
         quantise(6)
-        o_affine_bank = new_bank().bitcast(BF16)[:, 0:H]
-        for j in range(H // P):
-            block = slice(j * P, (j + 1) * P)
-            nc.tensor.transpose(o_affine_bank[:, block], o_affine_rows[:, block], ident_bf16[:])
-        o_affine = consts.tile([P, 2, H // P], F32)
-        nc.vector.tensor_copy(
-            out=o_affine[:],
-            in_=o_affine_bank.rearrange("p (j r) -> p r j", r=P)[:, 0:2, :],
-        )
-
-        mx_pass(6)
+        spread_transposes(CELL)
         apply_function(I_GATE, whole)
-        quantise(7)
-        mx_pass(7)
         for cols in halves:
             norm_finish(G_GATE, cols)
         for cols in halves:
             apply_function(G_GATE, cols)
+        quantise(7)
+        o_affine_bank = new_bank().bitcast(BF16)[:, 0:H]
+        for j in range(H // P):
+            block = slice(j * P, (j + 1) * P)
+            nc.tensor.transpose(o_affine_bank[:, block], affine_rows[:, block], ident_bf16[:])
+        o_affine = consts.tile([P, 2, H // P], F32)
 
-        norm_stats(O_GATE, acc[O_GATE][:])
-        norm_moments(O_GATE)
+        mx_gate(O_GATE)
+        spread_copy(CELL, nc.scalar.copy)
+
+
+        fresh = kept.tile([P, H], F32)
+        for cols in halves:
+            nc.vector.tensor_tensor(
+                out=fresh[:, cols], in0=gate[I_GATE][:, cols], in1=gate[G_GATE][:, cols], op=ALU.mult
+            )
+        norm_stats(O_GATE, acc[O_GATE], (whole,))
+        nc.vector.tensor_copy(
+            out=o_affine[:],
+            in_=o_affine_bank.rearrange("p (j r) -> p r j", r=P)[:, O_GATE : 2 * GATES : GATES, :],
+        )
+        cell = kept.tile([P, H], F32)
+        nc.vector.tensor_tensor(
+            out=cell[:, halves[0]], in0=held[:, halves[0]], in1=fresh[:, halves[0]], op=ALU.add
+        )
+        norm_mean(O_GATE)
+        nc.vector.tensor_tensor(
+            out=cell[:, halves[1]], in0=held[:, halves[1]], in1=fresh[:, halves[1]], op=ALU.add
+        )
+        norm_floor(O_GATE, nc.vector)
+        stats[CELL] = kept.tile([P, 2, 6], F32, name="stats_%d" % CELL)
+        nc.vector.bn_stats(out=stats[CELL][:, 0, :], in_=cell[:, halves[0]])
+        norm_rstd(O_GATE, nc.vector)
+        nc.vector.bn_stats(out=stats[CELL][:, 1, :], in_=cell[:, halves[1]])
         o_shift = kept.tile([P, 1], F32)
         nc.gpsimd.tensor_scalar(
             out=o_shift[:], in0=mean_var[O_GATE][:, 0:1], scalar1=rstd[O_GATE][:], scalar2=-1.0,
             op0=ALU.mult, op1=ALU.mult,
         )
-        fresh = kept.tile([P, H], F32)
-        nc.vector.tensor_tensor(out=fresh[:], in0=gate[I_GATE][:], in1=gate[G_GATE][:], op=ALU.mult)
-        cell = kept.tile([P, H], F32)
-        nc.vector.tensor_tensor(out=cell[:], in0=held[:], in1=fresh[:], op=ALU.add)
-        norm_stats(CELL, cell[:])
-        norm_moments(CELL)
-        norm_centre(CELL, cell[:])
+        norm_mean(CELL)
+        norm_floor(CELL, nc.vector)
+        norm_centre(CELL, cell, halves[0])
+        norm_rstd(CELL, nc.vector)
+        norm_centre(CELL, cell, halves[1])
 
         o_unit = kept.tile([P, H], F32)
-        nc.scalar.activation(
-            out=o_unit[:], in_=acc[O_GATE][:], func=ACT.Identity,
-            bias=o_shift[:], scale=rstd[O_GATE][:],
-        )
+        for cols in halves:
+            nc.scalar.activation(
+                out=o_unit[:, cols], in_=acc[O_GATE][:, cols], func=ACT.Identity,
+                bias=o_shift[:], scale=rstd[O_GATE][:],
+            )
         o_turned_bank = new_bank()
         o_turned = kept.tile([P, H], F32)
         o_bank = new_bank()

@@ -5,6 +5,7 @@ from concourse.masks import make_identity
 
 F32 = mybir.dt.float32
 BF16 = mybir.dt.bfloat16
+I32 = mybir.dt.int32
 U32 = mybir.dt.uint32
 U8 = mybir.dt.uint8
 FP8X4 = mybir.dt.float8_e4m3fn_x4
@@ -47,7 +48,7 @@ def tile_layernormdropoutlstmcell_s_kernel(
         sums = ctx.enter_context(tc.psum_pool(name="sums", bufs=2))
 
         affine_rows = inputs.tile([P, H], BF16)
-        nc.vector.memset(affine_rows[:], 0.0)
+        nc.vector.memset(affine_rows[:].bitcast(I32), 0)
         ident = consts.tile([P, P], F32)
         make_identity(nc, ident[:])
         ident_bf16 = consts.tile([P, P], BF16)
@@ -73,8 +74,10 @@ def tile_layernormdropoutlstmcell_s_kernel(
                 rows = inputs.tile([P, blocks * K], BF16, name="w_rows_%d_%d" % (u, part))
                 first = gate * H + part * blocks * P
                 nc.sync.dma_start(
-                    out=rows[:].rearrange("p (b k) -> p b k", b=blocks),
-                    in_=weight[first : first + blocks * P, :].rearrange("(b p) k -> p b k", p=P),
+                    out=rows[:].rearrange("p (h w) -> p h w", w=2 * K),
+                    in_=weight[first : first + blocks * P, :].rearrange(
+                        "(h p j) k -> p h (j k)", p=P, j=2
+                    ),
                 )
                 tiles.append(rows)
             w_rows.append((tiles, blocks))
@@ -108,19 +111,11 @@ def tile_layernormdropoutlstmcell_s_kernel(
             return bank[:]
 
         def new_planes():
-            return new_bank().rearrange("p (u c) -> p u c", u=2)
+            return new_bank().rearrange("p (j u r) -> p j u r", j=2, u=2)
 
-        def transpose_words(planes, column, rows_words):
+        def transpose_words(planes, rows_words):
             for u in range(2):
-                nc.tensor.transpose(
-                    planes[:, u, column : column + P], rows_words[:, u : WORDS : 2], ident[:]
-                )
-
-        def regroup(copy, grouped_words, planes):
-            copy(
-                out=grouped_words.rearrange("p (c u) -> p c u", u=2),
-                in_=planes.rearrange("p u c -> p c u"),
-            )
+                nc.tensor.transpose(planes[:, u, :], rows_words[:, u : WORDS : 2], ident[:])
 
         affine = {}
 
@@ -149,15 +144,20 @@ def tile_layernormdropoutlstmcell_s_kernel(
 
         def unit_to_k_major(u):
             grouped[u] = staging.tile([P, 4 * H], BF16, align_bytes=64, name="w_grouped")
-            grouped_words = grouped[u][:].bitcast(F32)
+            columns = grouped[u][:].bitcast(F32).rearrange(
+                "p (h r j u) -> p h r j u", h=2, j=2, u=2
+            )
             tiles, blocks = w_rows[u]
             for half in range(2):
                 planes = new_planes()
                 for j in range(2):
                     part, b = divmod(2 * half + j, blocks)
                     rows_words = tiles[part][:].bitcast(F32)
-                    transpose_words(planes, j * P, rows_words[:, b * WORDS : (b + 1) * WORDS])
-                regroup(nc.scalar.copy, grouped_words[:, half * BANK : (half + 1) * BANK], planes)
+                    transpose_words(planes[:, j, :, :], rows_words[:, b * WORDS : (b + 1) * WORDS])
+                nc.scalar.copy(
+                    out=columns[:, half, :, :, :],
+                    in_=planes.rearrange("p j u r -> p r j u"),
+                )
 
         def quantise(u, parts=1):
             w_codes[u] = operands.tile([P, H], U32, align_bytes=64, name="w_codes_%d" % u)
@@ -251,22 +251,25 @@ def tile_layernormdropoutlstmcell_s_kernel(
                 bias=gate_bias[:, g : g + 1],
             )
 
-        planes = new_planes()
+        unit_to_k_major(0)
+        affine_bank = new_bank().rearrange("p (u r) -> p u r", r=P)
         affine_words = affine_rows[:].bitcast(F32)
         for u in range(2):
-            nc.tensor.transpose(planes[:, u, 0:P], affine_words[:, u * P : (u + 1) * P], ident[:])
+            nc.tensor.transpose(affine_bank[:, u, :], affine_words[:, u * P : (u + 1) * P], ident[:])
         affine_cols = consts.tile([P, 2, 2 * NORMS], F32)
-        nc.vector.tensor_copy(out=affine_cols[:], in_=planes[:, :, 0 : 2 * NORMS])
-        unit_to_k_major(0)
-        spread_transposes(F_GATE)
+        nc.vector.tensor_copy(out=affine_cols[:], in_=affine_bank[:, 0:2, 0 : 2 * NORMS])
         unit_to_k_major(1)
+        spread_transposes(F_GATE)
         quantise(0)
         spread_copy(F_GATE, nc.vector.tensor_copy)
         planes = new_planes()
-        transpose_words(planes, 0, x_rows[:].bitcast(F32))
-        transpose_words(planes, P, hx_rows[:].bitcast(F32))
+        transpose_words(planes[:, 0, :, :], x_rows[:].bitcast(F32))
+        transpose_words(planes[:, 1, :, :], hx_rows[:].bitcast(F32))
         act_grouped = staging.tile([P, 4 * 2 * P], BF16, align_bytes=64)
-        regroup(nc.vector.tensor_copy, act_grouped[:].bitcast(F32), planes)
+        nc.vector.tensor_copy(
+            out=act_grouped[:].bitcast(F32).rearrange("p (j r u) -> p j r u", j=2, u=2),
+            in_=planes.rearrange("p j u r -> p j r u"),
+        )
         act_codes = operands.tile([P, 2 * P], U32, align_bytes=64)
         act_scales = operands.tile([P, 2 * P], U8, align_bytes=64)
         quantise(1)

@@ -47,12 +47,8 @@ def tile_layernormdropoutlstmcell_s_kernel(
         banks = ctx.enter_context(tc.psum_pool(name="banks", bufs=6))
         sums = ctx.enter_context(tc.psum_pool(name="sums", bufs=2))
 
-        affine_rows = inputs.tile([P, H], BF16)
-        nc.vector.memset(affine_rows[:].bitcast(I32), 0)
         ident = consts.tile([P, P], F32)
         make_identity(nc, ident[:])
-        ident_bf16 = consts.tile([P, P], BF16)
-        nc.vector.tensor_copy(out=ident_bf16[:], in_=ident[:])
         minus_half = consts.tile([P, 1], F32)
         nc.gpsimd.memset(minus_half[:], -0.5)
         gate_bias = consts.tile([P, GATES], F32)
@@ -82,29 +78,37 @@ def tile_layernormdropoutlstmcell_s_kernel(
                 tiles.append(rows)
             w_rows.append((tiles, blocks))
 
-        gamma_row = (0, 1, 2, 3, 8)
-        beta_row = (4, 5, 6, 7, 9)
-        for first, last, row in ((0, GATES, 0), (CELL, NORMS, 2 * GATES)):
-            count = last - first
-            nc.scalar.dma_start(out=affine_rows[row : row + count, :], in_=gamma[first:last, :])
-            nc.scalar.dma_start(
-                out=affine_rows[row + count : row + 2 * count, :], in_=beta[first:last, :]
-            )
+        affine = {}
 
-        table_warm = consts.tile([P, 1], F32)
-        nc.scalar.activation(out=table_warm[:], in_=minus_half[:], func=ACT.Sigmoid)
+        def load_affine(first, count):
+            for name, source in (("gamma", gamma), ("beta", beta)):
+                spread = consts.tile([P, count * H], BF16, name="%s_%d" % (name, first))
+                nc.sync.dma_start(
+                    out=spread[:],
+                    in_=source[first : first + count, :]
+                    .rearrange("n h -> (n h)")
+                    .partition_broadcast(P),
+                )
+                for n in range(count):
+                    affine[name, first + n] = spread[:, n * H : (n + 1) * H]
 
         load_unit(2)
-        load_unit(1)
         nc.sync.dma_start(out=x_rows[:], in_=x[:, :])
         nc.sync.dma_start(out=hx_rows[:], in_=hx[:, :])
         load_unit(1)
         load_unit(1)
         load_unit(1)
         load_unit(1)
+        load_affine(I_GATE, 2)
+        load_unit(1)
         nc.sync.dma_start(out=cx_rows[:], in_=cx[:, :])
         load_unit(1)
+        load_affine(G_GATE, 1)
         load_unit(1)
+        load_affine(O_GATE, 2)
+
+        table_warm = consts.tile([P, 1], F32)
+        nc.scalar.activation(out=table_warm[:], in_=minus_half[:], func=ACT.Sigmoid)
 
         def new_bank():
             bank = banks.tile([P, BANK], F32, name="bank")
@@ -116,27 +120,6 @@ def tile_layernormdropoutlstmcell_s_kernel(
         def transpose_words(planes, rows_words):
             for u in range(2):
                 nc.tensor.transpose(planes[:, u, :], rows_words[:, u : WORDS : 2], ident[:])
-
-        affine = {}
-
-        spread_bank = {}
-
-        def spread_transposes(n):
-            spread_bank[n] = new_bank()
-            for s, row in enumerate((gamma_row[n], beta_row[n])):
-                for u in range(2):
-                    column = (2 * s + u) * P
-                    nc.tensor.transpose(
-                        spread_bank[n][:, column : column + P],
-                        affine_cols[:, u, row : row + 1].to_broadcast([P, P]),
-                        ident[:],
-                    )
-
-        def spread_copy(n, copy):
-            spread = consts.tile([P, 2 * H], BF16, name="affine_%d" % n)
-            copy(out=spread[:].bitcast(F32), in_=spread_bank[n])
-            affine["gamma", n] = spread[:, 0:H]
-            affine["beta", n] = spread[:, H : 2 * H]
 
         grouped = {}
         w_codes = {}
@@ -159,7 +142,7 @@ def tile_layernormdropoutlstmcell_s_kernel(
                     in_=planes.rearrange("p j u r -> p r j u"),
                 )
 
-        def quantise(u, parts=1):
+        def quantise(u, parts=1, between=None, n=None):
             w_codes[u] = operands.tile([P, H], U32, align_bytes=64, name="w_codes_%d" % u)
             w_scales[u] = operands.tile([P, H], U8, align_bytes=64, name="w_scales_%d" % u)
             width = H // parts
@@ -169,6 +152,8 @@ def tile_layernormdropoutlstmcell_s_kernel(
                     out=w_codes[u][:, cols].bitcast(FP8X4), scales=w_scales[u][:, cols],
                     in_=grouped[u][:, 4 * part * width : 4 * (part + 1) * width],
                 )
+                if part == 0 and between is not None:
+                    between(n)
 
         acc = {}
 
@@ -252,16 +237,6 @@ def tile_layernormdropoutlstmcell_s_kernel(
             )
 
         unit_to_k_major(0)
-        affine_bank = new_bank().rearrange("p (u r) -> p u r", r=P)
-        affine_words = affine_rows[:].bitcast(F32)
-        for u in range(2):
-            nc.tensor.transpose(affine_bank[:, u, :], affine_words[:, u * P : (u + 1) * P], ident[:])
-        affine_cols = consts.tile([P, 2, 2 * NORMS], F32)
-        nc.vector.tensor_copy(out=affine_cols[:], in_=affine_bank[:, 0:2, 0 : 2 * NORMS])
-        unit_to_k_major(1)
-        spread_transposes(F_GATE)
-        quantise(0)
-        spread_copy(F_GATE, nc.vector.tensor_copy)
         planes = new_planes()
         transpose_words(planes[:, 0, :, :], x_rows[:].bitcast(F32))
         transpose_words(planes[:, 1, :, :], hx_rows[:].bitcast(F32))
@@ -270,16 +245,16 @@ def tile_layernormdropoutlstmcell_s_kernel(
             out=act_grouped[:].bitcast(F32).rearrange("p (j r u) -> p j r u", j=2, u=2),
             in_=planes.rearrange("p j u r -> p j r u"),
         )
+        quantise(0)
+        unit_to_k_major(1)
         act_codes = operands.tile([P, 2 * P], U32, align_bytes=64)
         act_scales = operands.tile([P, 2 * P], U8, align_bytes=64)
-        quantise(1)
         nc.vector.quantize_mx(
             out=act_codes[:].bitcast(FP8X4), scales=act_scales[:], in_=act_grouped[:]
         )
-        spread_transposes(I_GATE)
+        quantise(1)
         unit_to_k_major(2)
         mx_gate(F_GATE)
-        spread_copy(I_GATE, nc.vector.tensor_copy)
         quantise(2)
         norm_stats(F_GATE, acc[F_GATE], (whole,))
         unit_to_k_major(3)
@@ -293,17 +268,14 @@ def tile_layernormdropoutlstmcell_s_kernel(
         quantise(4)
         norm_finish(F_GATE, whole)
         norm_stats(I_GATE, acc[I_GATE], (whole,))
-        norm_mean(I_GATE)
+        unit_to_k_major(5)
+        apply_function(F_GATE, whole)
+        quantise(5, 2, norm_mean, I_GATE)
         norm_floor(I_GATE, nc.gpsimd)
         norm_rstd(I_GATE, nc.gpsimd)
-        unit_to_k_major(5)
-        spread_transposes(G_GATE)
-        quantise(5, 2)
         mx_gate(G_GATE, 2)
-        spread_copy(G_GATE, nc.scalar.copy)
-        apply_function(F_GATE, whole)
-        unit_to_k_major(6)
         norm_centre(I_GATE, acc[I_GATE], whole)
+        unit_to_k_major(6)
         held = kept.tile([P, H], F32)
         nc.gpsimd.tensor_tensor(out=held[:], in0=gate[F_GATE][:], in1=cx_rows[:], op=ALU.mult)
 
@@ -315,78 +287,34 @@ def tile_layernormdropoutlstmcell_s_kernel(
         norm_centre(G_GATE, acc[G_GATE], whole)
         norm_rstd(G_GATE, nc.vector)
         quantise(6)
-        spread_transposes(CELL)
         apply_function(I_GATE, whole)
         for cols in halves:
             norm_finish(G_GATE, cols)
         for cols in halves:
             apply_function(G_GATE, cols)
         quantise(7)
-        o_affine_bank = new_bank().bitcast(BF16)[:, 0:H]
-        for j in range(H // P):
-            block = slice(j * P, (j + 1) * P)
-            nc.tensor.transpose(o_affine_bank[:, block], affine_rows[:, block], ident_bf16[:])
-        o_affine = consts.tile([P, 2, H // P], F32)
-
         mx_gate(O_GATE)
-        spread_copy(CELL, nc.scalar.copy)
-
-
         fresh = kept.tile([P, H], F32)
+        cell = kept.tile([P, H], F32)
         for cols in halves:
             nc.vector.tensor_tensor(
                 out=fresh[:, cols], in0=gate[I_GATE][:, cols], in1=gate[G_GATE][:, cols], op=ALU.mult
             )
+        for cols in halves:
+            nc.vector.tensor_tensor(
+                out=cell[:, cols], in0=held[:, cols], in1=fresh[:, cols], op=ALU.add
+            )
         norm_stats(O_GATE, acc[O_GATE], (whole,))
-        nc.vector.tensor_copy(
-            out=o_affine[:],
-            in_=o_affine_bank.rearrange("p (j r) -> p r j", r=P)[:, O_GATE : 2 * GATES : GATES, :],
-        )
-        cell = kept.tile([P, H], F32)
-        nc.vector.tensor_tensor(
-            out=cell[:, halves[0]], in0=held[:, halves[0]], in1=fresh[:, halves[0]], op=ALU.add
-        )
+        norm_stats(CELL, cell, halves)
         norm_mean(O_GATE)
-        nc.vector.tensor_tensor(
-            out=cell[:, halves[1]], in0=held[:, halves[1]], in1=fresh[:, halves[1]], op=ALU.add
-        )
-        norm_floor(O_GATE, nc.vector)
-        stats[CELL] = kept.tile([P, 2, 6], F32, name="stats_%d" % CELL)
-        nc.vector.bn_stats(out=stats[CELL][:, 0, :], in_=cell[:, halves[0]])
-        norm_rstd(O_GATE, nc.vector)
-        nc.vector.bn_stats(out=stats[CELL][:, 1, :], in_=cell[:, halves[1]])
-        o_shift = kept.tile([P, 1], F32)
-        nc.gpsimd.tensor_scalar(
-            out=o_shift[:], in0=mean_var[O_GATE][:, 0:1], scalar1=rstd[O_GATE][:], scalar2=-1.0,
-            op0=ALU.mult, op1=ALU.mult,
-        )
         norm_mean(CELL)
+        norm_floor(O_GATE, nc.vector)
         norm_floor(CELL, nc.vector)
         norm_centre(CELL, cell, halves[0])
         norm_rstd(CELL, nc.vector)
+        norm_rstd(O_GATE, nc.vector)
         norm_centre(CELL, cell, halves[1])
-
-        o_unit = kept.tile([P, H], F32)
-        for cols in halves:
-            nc.scalar.activation(
-                out=o_unit[:, cols], in_=acc[O_GATE][:, cols], func=ACT.Identity,
-                bias=o_shift[:], scale=rstd[O_GATE][:],
-            )
-        o_turned_bank = new_bank()
-        o_turned = kept.tile([P, H], F32)
-        o_bank = new_bank()
-        for j in range(H // P):
-            block = slice(j * P, (j + 1) * P)
-            nc.tensor.transpose(o_turned_bank[:, block], o_unit[:, block], ident[:])
-        for j in range(H // P):
-            block = slice(j * P, (j + 1) * P)
-            nc.scalar.activation(
-                out=o_turned[:, block], in_=o_turned_bank[:, block], func=ACT.Sigmoid,
-                bias=o_affine[:, 1, j : j + 1], scale=o_affine[:, 0, j : j + 1],
-            )
-        for j in range(H // P):
-            block = slice(j * P, (j + 1) * P)
-            nc.tensor.transpose(o_bank[:, block], o_turned[:, block], ident[:])
+        norm_centre(O_GATE, acc[O_GATE], whole)
 
         tanh_cy = kept.tile([P, H], F32)
         hy = kept.tile([P, H], F32)
@@ -394,10 +322,14 @@ def tile_layernormdropoutlstmcell_s_kernel(
             norm_finish(CELL, cols)
         nc.sync.dma_start(out=out_2[:, :], in_=normed[CELL][:])
         for cols in halves:
+            norm_finish(O_GATE, cols)
+        for cols in halves:
             nc.scalar.activation(out=tanh_cy[:, cols], in_=normed[CELL][:, cols], func=ACT.Tanh)
         for cols in halves:
+            apply_function(O_GATE, cols)
+        for cols in halves:
             nc.vector.tensor_tensor(
-                out=hy[:, cols], in0=o_bank[:, cols], in1=tanh_cy[:, cols], op=ALU.mult
+                out=hy[:, cols], in0=gate[O_GATE][:, cols], in1=tanh_cy[:, cols], op=ALU.mult
             )
             nc.sync.dma_start(out=out_0[:, cols], in_=hy[:, cols])
             nc.sync.dma_start(out=out_1[:, cols], in_=hy[:, cols])

@@ -95,12 +95,13 @@ def tile_layernormdropoutlstmcell_s_kernel(
         load_unit(2)
         nc.sync.dma_start(out=x_rows[:], in_=x[:, :])
         nc.sync.dma_start(out=hx_rows[:], in_=hx[:, :])
+        load_unit(2)
+        load_unit(2)
+        load_unit(1)
+        load_affine(F_GATE, 1)
         load_unit(1)
         load_unit(1)
-        load_unit(1)
-        load_unit(1)
-        load_affine(I_GATE, 2)
-        load_unit(1)
+        load_affine(I_GATE, 1)
         nc.sync.dma_start(out=cx_rows[:], in_=cx[:, :])
         load_unit(1)
         load_affine(G_GATE, 1)
@@ -187,8 +188,36 @@ def tile_layernormdropoutlstmcell_s_kernel(
                 nc.vector.bn_stats(out=stats[n][:, part, :], in_=v[:, cols])
 
         def norm_mean(n):
-            mean_var[n] = kept.tile([P, 2], F32, name="mean_var_%d" % n)
-            nc.vector.bn_aggr(out=mean_var[n][:], in_=stats[n][:].rearrange("p s k -> p (s k)"))
+            if n == O_GATE or n == CELL:
+                mean_var[n] = last_mean_var[:, n - O_GATE, :]
+            else:
+                tile = kept.tile([P, 2], F32, name="mean_var_%d" % n)
+                mean_var[n] = tile[:]
+            nc.vector.bn_aggr(out=mean_var[n], in_=stats[n][:].rearrange("p s k -> p (s k)"))
+
+        last_mean_var = kept.tile([P, 2, 2], F32)
+        last_floor = kept.tile([P, 2], F32)
+        last_padded = kept.tile([P, 2], F32)
+        last_rstd = kept.tile([P, 2], F32)
+        minus_halves = consts.tile([P, 2], F32)
+        nc.gpsimd.memset(minus_halves[:], -0.5)
+
+        def last_norms_floor():
+            nc.vector.tensor_scalar(
+                out=last_floor[:], in0=last_mean_var[:, :, 1], scalar1=EPS, scalar2=VAR_FLOOR,
+                op0=ALU.is_lt, op1=ALU.mult,
+            )
+
+        def last_norms_rstd():
+            nc.vector.scalar_tensor_tensor(
+                out=last_padded[:], in0=last_floor[:], scalar=EPS, in1=last_mean_var[:, :, 1],
+                op0=ALU.add, op1=ALU.add,
+            )
+            nc.gpsimd.tensor_tensor(
+                out=last_rstd[:], in0=last_padded[:], in1=minus_halves[:], op=ALU.pow
+            )
+            for n in (O_GATE, CELL):
+                rstd[n] = last_rstd[:, n - O_GATE : n - O_GATE + 1]
 
         floor = {}
 
@@ -199,14 +228,21 @@ def tile_layernormdropoutlstmcell_s_kernel(
                 op0=ALU.is_lt, op1=ALU.mult,
             )
 
-        def norm_rstd(n, engine):
-            padded = kept.tile([P, 1], F32, name="padded_%d" % n)
+        padded = {}
+
+        def norm_padded(n, engine):
+            padded[n] = kept.tile([P, 1], F32, name="padded_%d" % n)
             engine.tensor_scalar(
-                out=padded[:], in0=floor[n][:], scalar1=mean_var[n][:, 1:2], scalar2=EPS,
+                out=padded[n][:], in0=floor[n][:], scalar1=mean_var[n][:, 1:2], scalar2=EPS,
                 op0=ALU.add, op1=ALU.add,
             )
-            rstd[n] = kept.tile([P, 1], F32, name="rstd_%d" % n)
-            nc.gpsimd.tensor_tensor(out=rstd[n][:], in0=padded[:], in1=minus_half[:], op=ALU.pow)
+
+        def norm_rstd(n):
+            tile = kept.tile([P, 1], F32, name="rstd_%d" % n)
+            rstd[n] = tile[:]
+            nc.gpsimd.tensor_tensor(
+                out=rstd[n], in0=padded[n][:], in1=minus_half[:], op=ALU.pow
+            )
 
         def norm_centre(n, v, cols):
             if n not in centred:
@@ -222,7 +258,7 @@ def tile_layernormdropoutlstmcell_s_kernel(
             if n not in normed:
                 normed[n] = kept.tile([P, H], F32, name="normed_%d" % n)
             nc.vector.scalar_tensor_tensor(
-                out=normed[n][:, cols], in0=centred[n][:, cols], scalar=rstd[n][:],
+                out=normed[n][:, cols], in0=centred[n][:, cols], scalar=rstd[n],
                 in1=affine["beta", n][:, cols], op0=ALU.mult, op1=ALU.add,
             )
 
@@ -260,32 +296,36 @@ def tile_layernormdropoutlstmcell_s_kernel(
         unit_to_k_major(3)
         norm_mean(F_GATE)
         norm_floor(F_GATE, nc.gpsimd)
-        norm_rstd(F_GATE, nc.gpsimd)
-        quantise(3)
+        norm_padded(F_GATE, nc.gpsimd)
+        norm_rstd(F_GATE)
         norm_centre(F_GATE, acc[F_GATE], whole)
+        quantise(3)
         unit_to_k_major(4)
         mx_gate(I_GATE)
-        quantise(4)
         norm_finish(F_GATE, whole)
+        quantise(4)
         norm_stats(I_GATE, acc[I_GATE], (whole,))
         unit_to_k_major(5)
         apply_function(F_GATE, whole)
         quantise(5, 2, norm_mean, I_GATE)
         norm_floor(I_GATE, nc.gpsimd)
-        norm_rstd(I_GATE, nc.gpsimd)
-        mx_gate(G_GATE, 2)
-        norm_centre(I_GATE, acc[I_GATE], whole)
-        unit_to_k_major(6)
+        norm_padded(I_GATE, nc.gpsimd)
         held = kept.tile([P, H], F32)
         nc.gpsimd.tensor_tensor(out=held[:], in0=gate[F_GATE][:], in1=cx_rows[:], op=ALU.mult)
+        norm_rstd(I_GATE)
+        mx_gate(G_GATE, 2)
+        unit_to_k_major(6)
 
         unit_to_k_major(7)
         norm_stats(G_GATE, acc[G_GATE], halves)
-        norm_finish(I_GATE, whole)
+        norm_centre(I_GATE, acc[I_GATE], halves[0])
         norm_mean(G_GATE)
+        norm_centre(I_GATE, acc[I_GATE], halves[1])
         norm_floor(G_GATE, nc.vector)
         norm_centre(G_GATE, acc[G_GATE], whole)
-        norm_rstd(G_GATE, nc.vector)
+        norm_padded(G_GATE, nc.vector)
+        norm_rstd(G_GATE)
+        norm_finish(I_GATE, whole)
         quantise(6)
         apply_function(I_GATE, whole)
         for cols in halves:
@@ -308,11 +348,9 @@ def tile_layernormdropoutlstmcell_s_kernel(
         norm_stats(CELL, cell, halves)
         norm_mean(O_GATE)
         norm_mean(CELL)
-        norm_floor(O_GATE, nc.vector)
-        norm_floor(CELL, nc.vector)
+        last_norms_floor()
         norm_centre(CELL, cell, halves[0])
-        norm_rstd(CELL, nc.vector)
-        norm_rstd(O_GATE, nc.vector)
+        last_norms_rstd()
         norm_centre(CELL, cell, halves[1])
         norm_centre(O_GATE, acc[O_GATE], whole)
 
@@ -320,12 +358,9 @@ def tile_layernormdropoutlstmcell_s_kernel(
         hy = kept.tile([P, H], F32)
         for cols in halves:
             norm_finish(CELL, cols)
-        nc.sync.dma_start(out=out_2[:, :], in_=normed[CELL][:])
-        for cols in halves:
-            norm_finish(O_GATE, cols)
-        for cols in halves:
+            nc.sync.dma_start(out=out_2[:, cols], in_=normed[CELL][:, cols])
             nc.scalar.activation(out=tanh_cy[:, cols], in_=normed[CELL][:, cols], func=ACT.Tanh)
-        for cols in halves:
+            norm_finish(O_GATE, cols)
             apply_function(O_GATE, cols)
         for cols in halves:
             nc.vector.tensor_tensor(

@@ -98,8 +98,8 @@ def tile_layernormdropoutlstmcell_s_kernel(
         load_unit(2)
         load_unit(2)
         load_unit(1)
-        load_affine(F_GATE, 1)
         load_unit(1)
+        load_affine(F_GATE, 1)
         load_unit(1)
         load_affine(I_GATE, 1)
         nc.sync.dma_start(out=cx_rows[:], in_=cx[:, :])
@@ -298,12 +298,12 @@ def tile_layernormdropoutlstmcell_s_kernel(
         norm_floor(F_GATE, nc.gpsimd)
         norm_padded(F_GATE, nc.gpsimd)
         norm_rstd(F_GATE)
-        norm_centre(F_GATE, acc[F_GATE], whole)
         quantise(3)
+        norm_centre(F_GATE, acc[F_GATE], whole)
         unit_to_k_major(4)
         mx_gate(I_GATE)
-        norm_finish(F_GATE, whole)
         quantise(4)
+        norm_finish(F_GATE, whole)
         norm_stats(I_GATE, acc[I_GATE], (whole,))
         unit_to_k_major(5)
         apply_function(F_GATE, whole)

@@ -1,3 +1,4 @@
+import math
 from contextlib import ExitStack
 
 import concourse.mybir as mybir
@@ -29,6 +30,7 @@ NORMS = GATES + 1
 EPS = 1e-12
 VAR_FLOOR = 0.01
 FORGET_BIAS = 1.0
+ROOT_H = math.sqrt(H)
 
 FLOPS = 2 * P * (GATES * H) * (2 * K)
 
@@ -97,7 +99,7 @@ def tile_layernormdropoutlstmcell_s_kernel(
         nc.sync.dma_start(out=hx_rows[:], in_=hx[:, :])
         load_unit(2)
         load_unit(2)
-        load_unit(1)
+        load_unit(2)
         load_unit(1)
         load_affine(F_GATE, 1)
         load_unit(1)
@@ -187,37 +189,73 @@ def tile_layernormdropoutlstmcell_s_kernel(
             for part, cols in enumerate(parts):
                 nc.vector.bn_stats(out=stats[n][:, part, :], in_=v[:, cols])
 
+        mean_var_of = {}
+        PAIRS = ((I_GATE, G_GATE), (O_GATE, CELL))
+        pair_mean_var = {}
+        pair_floor = {}
+        minus_halves = consts.tile([P, 2], F32)
+        nc.gpsimd.memset(minus_halves[:], -0.5)
+        for pair in PAIRS:
+            pair_mean_var[pair] = kept.tile([P, 2, 2], F32, name="mean_var_%d_%d" % pair)
+            for slot, n in enumerate(pair):
+                mean_var[n] = pair_mean_var[pair][:, slot, :]
+
+        def pair_norms_floor(pair):
+            pair_floor[pair] = kept.tile([P, 2], F32, name="floor_%d_%d" % pair)
+            nc.vector.tensor_scalar(
+                out=pair_floor[pair][:], in0=pair_mean_var[pair][:, :, 1], scalar1=EPS,
+                scalar2=VAR_FLOOR, op0=ALU.is_lt, op1=ALU.mult,
+            )
+
+        def pair_norms_rstd(pair):
+            pair_padded = kept.tile([P, 2], F32, name="padded_%d_%d" % pair)
+            nc.vector.scalar_tensor_tensor(
+                out=pair_padded[:], in0=pair_floor[pair][:], scalar=EPS,
+                in1=pair_mean_var[pair][:, :, 1], op0=ALU.add, op1=ALU.add,
+            )
+            pair_rstd = kept.tile([P, 2], F32, name="rstd_%d_%d" % pair)
+            nc.gpsimd.tensor_tensor(
+                out=pair_rstd[:], in0=pair_padded[:], in1=minus_halves[:], op=ALU.pow
+            )
+            for slot, n in enumerate(pair):
+                rstd[n] = pair_rstd[:, slot : slot + 1]
+
         def norm_mean(n):
-            if n == O_GATE or n == CELL:
-                mean_var[n] = last_mean_var[:, n - O_GATE, :]
-            else:
+            if n not in mean_var:
                 tile = kept.tile([P, 2], F32, name="mean_var_%d" % n)
                 mean_var[n] = tile[:]
             nc.vector.bn_aggr(out=mean_var[n], in_=stats[n][:].rearrange("p s k -> p (s k)"))
 
-        last_mean_var = kept.tile([P, 2, 2], F32)
-        last_floor = kept.tile([P, 2], F32)
-        last_padded = kept.tile([P, 2], F32)
-        last_rstd = kept.tile([P, 2], F32)
-        minus_halves = consts.tile([P, 2], F32)
-        nc.gpsimd.memset(minus_halves[:], -0.5)
+        passed = {}
+        shift = {}
+        minus_mean = {}
 
-        def last_norms_floor():
-            nc.vector.tensor_scalar(
-                out=last_floor[:], in0=last_mean_var[:, :, 1], scalar1=EPS, scalar2=VAR_FLOOR,
-                op0=ALU.is_lt, op1=ALU.mult,
+        def scalar_sum(n, v):
+            passed[n] = kept.tile([P, H], F32, name="passed_%d" % n)
+            shift[n] = kept.tile([P, 1], F32, name="shift_%d" % n)
+            nc.scalar.activation(
+                out=passed[n][:], in_=v, func=ACT.Identity, scale=-1.0 / (H * ROOT_H),
+                accum_out=shift[n][:],
+            )
+            minus_mean[n] = kept.tile([P, 1], F32, name="minus_mean_%d" % n)
+            nc.gpsimd.tensor_scalar(
+                out=minus_mean[n][:], in0=shift[n][:], scalar1=ROOT_H, scalar2=0.0,
+                op0=ALU.mult, op1=ALU.add,
             )
 
-        def last_norms_rstd():
+        def scalar_var(n):
+            nc.scalar.activation(
+                out=passed[n][:], in_=passed[n][:], func=ACT.Square, scale=-float(H),
+                bias=shift[n][:], accum_out=mean_var[n][:, 1:2],
+            )
+
+        def centre_scalar(n, v, cols):
+            if n not in centred:
+                centred[n] = kept.tile([P, H], F32, name="centred_%d" % n)
             nc.vector.scalar_tensor_tensor(
-                out=last_padded[:], in0=last_floor[:], scalar=EPS, in1=last_mean_var[:, :, 1],
-                op0=ALU.add, op1=ALU.add,
+                out=centred[n][:, cols], in0=v[:, cols], scalar=minus_mean[n][:],
+                in1=affine["gamma", n][:, cols], op0=ALU.add, op1=ALU.mult,
             )
-            nc.gpsimd.tensor_tensor(
-                out=last_rstd[:], in0=last_padded[:], in1=minus_halves[:], op=ALU.pow
-            )
-            for n in (O_GATE, CELL):
-                rstd[n] = last_rstd[:, n - O_GATE : n - O_GATE + 1]
 
         floor = {}
 
@@ -295,42 +333,38 @@ def tile_layernormdropoutlstmcell_s_kernel(
         norm_stats(F_GATE, acc[F_GATE], (whole,))
         unit_to_k_major(3)
         norm_mean(F_GATE)
-        norm_floor(F_GATE, nc.gpsimd)
-        norm_padded(F_GATE, nc.gpsimd)
+        norm_floor(F_GATE, nc.vector)
+        quantise(3, 2, lambda n: norm_padded(n, nc.vector), F_GATE)
         norm_rstd(F_GATE)
-        quantise(3)
-        norm_centre(F_GATE, acc[F_GATE], whole)
+        for cols in halves:
+            norm_centre(F_GATE, acc[F_GATE], cols)
         unit_to_k_major(4)
-        mx_gate(I_GATE)
-        quantise(4)
-        norm_finish(F_GATE, whole)
-        norm_stats(I_GATE, acc[I_GATE], (whole,))
         unit_to_k_major(5)
+        mx_gate(I_GATE)
+        norm_finish(F_GATE, halves[0])
+        quantise(4)
+        norm_finish(F_GATE, halves[1])
+        quantise(5, 2)
+        mx_gate(G_GATE, 2)
         apply_function(F_GATE, whole)
-        quantise(5, 2, norm_mean, I_GATE)
-        norm_floor(I_GATE, nc.gpsimd)
-        norm_padded(I_GATE, nc.gpsimd)
         held = kept.tile([P, H], F32)
         nc.gpsimd.tensor_tensor(out=held[:], in0=gate[F_GATE][:], in1=cx_rows[:], op=ALU.mult)
-        norm_rstd(I_GATE)
-        mx_gate(G_GATE, 2)
         unit_to_k_major(6)
-
         unit_to_k_major(7)
+        norm_stats(I_GATE, acc[I_GATE], (whole,))
         norm_stats(G_GATE, acc[G_GATE], halves)
-        norm_centre(I_GATE, acc[I_GATE], halves[0])
+        norm_mean(I_GATE)
         norm_mean(G_GATE)
+        norm_centre(I_GATE, acc[I_GATE], halves[0])
+        pair_norms_floor(PAIRS[0])
         norm_centre(I_GATE, acc[I_GATE], halves[1])
-        norm_floor(G_GATE, nc.vector)
+        pair_norms_rstd(PAIRS[0])
         norm_centre(G_GATE, acc[G_GATE], whole)
-        norm_padded(G_GATE, nc.vector)
-        norm_rstd(G_GATE)
-        norm_finish(I_GATE, whole)
         quantise(6)
+        norm_finish(I_GATE, whole)
         apply_function(I_GATE, whole)
         for cols in halves:
             norm_finish(G_GATE, cols)
-        for cols in halves:
             apply_function(G_GATE, cols)
         quantise(7)
         mx_gate(O_GATE)
@@ -344,16 +378,15 @@ def tile_layernormdropoutlstmcell_s_kernel(
             nc.vector.tensor_tensor(
                 out=cell[:, cols], in0=held[:, cols], in1=fresh[:, cols], op=ALU.add
             )
-        norm_stats(O_GATE, acc[O_GATE], (whole,))
+        scalar_sum(O_GATE, acc[O_GATE][:])
+        scalar_var(O_GATE)
         norm_stats(CELL, cell, halves)
-        norm_mean(O_GATE)
         norm_mean(CELL)
-        last_norms_floor()
         norm_centre(CELL, cell, halves[0])
-        last_norms_rstd()
+        pair_norms_floor(PAIRS[1])
         norm_centre(CELL, cell, halves[1])
-        norm_centre(O_GATE, acc[O_GATE], whole)
-
+        pair_norms_rstd(PAIRS[1])
+        centre_scalar(O_GATE, acc[O_GATE], whole)
         tanh_cy = kept.tile([P, H], F32)
         hy = kept.tile([P, H], F32)
         for cols in halves:

@@ -82,8 +82,9 @@ def tile_layernormdropoutlstmcell_s_kernel(
 
         affine = {}
 
-        def load_affine(first, count):
-            for name, source in (("gamma", gamma), ("beta", beta)):
+        def load_affine(first, count, names=("gamma", "beta")):
+            for name in names:
+                source = {"gamma": gamma, "beta": beta}[name]
                 spread = consts.tile([P, count * H], BF16, name="%s_%d" % (name, first))
                 nc.sync.dma_start(
                     out=spread[:],
@@ -101,8 +102,9 @@ def tile_layernormdropoutlstmcell_s_kernel(
         load_unit(2)
         load_unit(2)
         load_unit(1)
-        load_affine(F_GATE, 1)
+        load_affine(F_GATE, 1, ("gamma",))
         load_unit(1)
+        load_affine(F_GATE, 1, ("beta",))
         load_affine(I_GATE, 1)
         nc.sync.dma_start(out=cx_rows[:], in_=cx[:, :])
         load_unit(1)
@@ -382,11 +384,12 @@ def tile_layernormdropoutlstmcell_s_kernel(
         scalar_var(O_GATE)
         norm_stats(CELL, cell, halves)
         norm_mean(CELL)
-        norm_centre(CELL, cell, halves[0])
+        centre_scalar(O_GATE, acc[O_GATE], halves[0])
         pair_norms_floor(PAIRS[1])
-        norm_centre(CELL, cell, halves[1])
+        norm_centre(CELL, cell, halves[0])
         pair_norms_rstd(PAIRS[1])
-        centre_scalar(O_GATE, acc[O_GATE], whole)
+        centre_scalar(O_GATE, acc[O_GATE], halves[1])
+        norm_centre(CELL, cell, halves[1])
         tanh_cy = kept.tile([P, H], F32)
         hy = kept.tile([P, H], F32)
         for cols in halves:

@@ -105,11 +105,13 @@ def tile_layernormdropoutlstmcell_s_kernel(
         load_affine(F_GATE, 1, ("gamma",))
         load_unit(1)
         load_affine(F_GATE, 1, ("beta",))
-        load_affine(I_GATE, 1)
         nc.sync.dma_start(out=cx_rows[:], in_=cx[:, :])
+        load_affine(I_GATE, 1, ("gamma",))
         load_unit(1)
-        load_affine(G_GATE, 1)
+        load_affine(I_GATE, 1, ("beta",))
+        load_affine(G_GATE, 1, ("gamma",))
         load_unit(1)
+        load_affine(G_GATE, 1, ("beta",))
         load_affine(O_GATE, 2)
 
         table_warm = consts.tile([P, 1], F32)
@@ -186,10 +188,11 @@ def tile_layernormdropoutlstmcell_s_kernel(
         rstd = {}
         centred = {}
 
-        def norm_stats(n, v, parts):
-            stats[n] = kept.tile([P, len(parts), 6], F32, name="stats_%d" % n)
+        def norm_stats(n, v, parts, first=0, count=None):
+            if first == 0:
+                stats[n] = kept.tile([P, count or len(parts), 6], F32, name="stats_%d" % n)
             for part, cols in enumerate(parts):
-                nc.vector.bn_stats(out=stats[n][:, part, :], in_=v[:, cols])
+                nc.vector.bn_stats(out=stats[n][:, first + part, :], in_=v[:, cols])
 
         mean_var_of = {}
         PAIRS = ((I_GATE, G_GATE), (O_GATE, CELL))
@@ -343,9 +346,8 @@ def tile_layernormdropoutlstmcell_s_kernel(
         unit_to_k_major(4)
         unit_to_k_major(5)
         mx_gate(I_GATE)
-        norm_finish(F_GATE, halves[0])
         quantise(4)
-        norm_finish(F_GATE, halves[1])
+        norm_finish(F_GATE, whole)
         quantise(5, 2)
         mx_gate(G_GATE, 2)
         apply_function(F_GATE, whole)
@@ -354,14 +356,16 @@ def tile_layernormdropoutlstmcell_s_kernel(
         unit_to_k_major(6)
         unit_to_k_major(7)
         norm_stats(I_GATE, acc[I_GATE], (whole,))
-        norm_stats(G_GATE, acc[G_GATE], halves)
+        norm_stats(G_GATE, acc[G_GATE], halves[:1], 0, 2)
         norm_mean(I_GATE)
-        norm_mean(G_GATE)
+        norm_stats(G_GATE, acc[G_GATE], halves[1:], 1)
         norm_centre(I_GATE, acc[I_GATE], halves[0])
-        pair_norms_floor(PAIRS[0])
+        norm_mean(G_GATE)
         norm_centre(I_GATE, acc[I_GATE], halves[1])
+        pair_norms_floor(PAIRS[0])
+        norm_centre(G_GATE, acc[G_GATE], halves[0])
         pair_norms_rstd(PAIRS[0])
-        norm_centre(G_GATE, acc[G_GATE], whole)
+        norm_centre(G_GATE, acc[G_GATE], halves[1])
         quantise(6)
         norm_finish(I_GATE, whole)
         apply_function(I_GATE, whole)

import math
from contextlib import ExitStack

import concourse.mybir as mybir
from concourse.masks import make_identity

F32 = mybir.dt.float32
BF16 = mybir.dt.bfloat16
I32 = mybir.dt.int32
U32 = mybir.dt.uint32
U8 = mybir.dt.uint8
FP8X4 = mybir.dt.float8_e4m3fn_x4
ALU = mybir.AluOpType
ACT = mybir.ActivationFunctionType

P = 128
K = 512
H = 512
BANK = 512
WORDS = K // 2
ROW_BLOCKS = H // P
I_GATE = 0
F_GATE = 1
G_GATE = 2
O_GATE = 3
CELL = 4
ORDER = (F_GATE, I_GATE, G_GATE, O_GATE)
GATES = len(ORDER)
NORMS = GATES + 1
EPS = 1e-12
VAR_FLOOR = 0.01
FORGET_BIAS = 1.0
ROOT_H = math.sqrt(H)

FLOPS = 2 * P * (GATES * H) * (2 * K)


def tile_layernormdropoutlstmcell_s_kernel(
    tc, x, hx, cx, weight_ih, weight_hh, gamma, beta, out_0, out_1, out_2
):
    nc = tc.nc
    with ExitStack() as ctx:
        ctx.enter_context(tc.manual_schedule())
        consts = ctx.enter_context(tc.tile_pool(name="consts", bufs=1))
        inputs = ctx.enter_context(tc.tile_pool(name="inputs", bufs=1))
        staging = ctx.enter_context(tc.tile_pool(name="staging", bufs=4))
        operands = ctx.enter_context(tc.tile_pool(name="operands", bufs=1))
        kept = ctx.enter_context(tc.tile_pool(name="kept", bufs=1))
        banks = ctx.enter_context(tc.psum_pool(name="banks", bufs=6))
        sums = ctx.enter_context(tc.psum_pool(name="sums", bufs=2))

        ident = consts.tile([P, P], F32)
        make_identity(nc, ident[:])
        minus_half = consts.tile([P, 1], F32)
        nc.gpsimd.memset(minus_half[:], -0.5)
        gate_bias = consts.tile([P, GATES], F32)
        nc.gpsimd.memset(gate_bias[:], 0.0)
        nc.gpsimd.memset(gate_bias[:, F_GATE : F_GATE + 1], FORGET_BIAS)
        gate_func = (ACT.Sigmoid, ACT.Sigmoid, ACT.Tanh, ACT.Sigmoid)

        x_rows = inputs.tile([P, K], BF16)
        hx_rows = inputs.tile([P, K], BF16)
        cx_rows = inputs.tile([P, H], BF16)
        w_rows = []

        def load_unit(parts):
            u = len(w_rows)
            gate, weight = ORDER[u // 2], (weight_ih, weight_hh)[u % 2]
            blocks = ROW_BLOCKS // parts
            tiles = []
            for part in range(parts):
                rows = inputs.tile([P, blocks * K], BF16, name="w_rows_%d_%d" % (u, part))
                first = gate * H + part * blocks * P
                nc.sync.dma_start(
                    out=rows[:].rearrange("p (h w) -> p h w", w=2 * K),
                    in_=weight[first : first + blocks * P, :].rearrange(
                        "(h p j) k -> p h (j k)", p=P, j=2
                    ),
                )
                tiles.append(rows)
            w_rows.append((tiles, blocks))

        affine = {}

        def load_affine(first, count, names=("gamma", "beta")):
            for name in names:
                source = {"gamma": gamma, "beta": beta}[name]
                spread = consts.tile([P, count * H], BF16, name="%s_%d" % (name, first))
                nc.sync.dma_start(
                    out=spread[:],
                    in_=source[first : first + count, :]
                    .rearrange("n h -> (n h)")
                    .partition_broadcast(P),
                )
                for n in range(count):
                    affine[name, first + n] = spread[:, n * H : (n + 1) * H]

        load_unit(2)
        nc.sync.dma_start(out=x_rows[:], in_=x[:, :])
        nc.sync.dma_start(out=hx_rows[:], in_=hx[:, :])
        load_unit(2)
        load_unit(2)
        load_unit(2)
        load_unit(1)
        load_affine(F_GATE, 1, ("gamma",))
        load_unit(1)
        load_affine(F_GATE, 1, ("beta",))
        nc.sync.dma_start(out=cx_rows[:], in_=cx[:, :])
        load_affine(I_GATE, 1, ("gamma",))
        load_unit(1)
        load_affine(I_GATE, 1, ("beta",))
        load_affine(G_GATE, 1, ("gamma",))
        load_unit(1)
        load_affine(G_GATE, 1, ("beta",))
        load_affine(O_GATE, 2)

        table_warm = consts.tile([P, 1], F32)
        nc.scalar.activation(out=table_warm[:], in_=minus_half[:], func=ACT.Sigmoid)

        def new_bank():
            bank = banks.tile([P, BANK], F32, name="bank")
            return bank[:]

        def new_planes():
            return new_bank().rearrange("p (j u r) -> p j u r", j=2, u=2)

        def transpose_words(planes, rows_words):
            for u in range(2):
                nc.tensor.transpose(planes[:, u, :], rows_words[:, u : WORDS : 2], ident[:])

        grouped = {}
        w_codes = {}
        w_scales = {}

        def unit_to_k_major(u):
            grouped[u] = staging.tile([P, 4 * H], BF16, align_bytes=64, name="w_grouped")
            columns = grouped[u][:].bitcast(F32).rearrange(
                "p (h r j u) -> p h r j u", h=2, j=2, u=2
            )
            tiles, blocks = w_rows[u]
            for half in range(2):
                planes = new_planes()
                for j in range(2):
                    part, b = divmod(2 * half + j, blocks)
                    rows_words = tiles[part][:].bitcast(F32)
                    transpose_words(planes[:, j, :, :], rows_words[:, b * WORDS : (b + 1) * WORDS])
                nc.scalar.copy(
                    out=columns[:, half, :, :, :],
                    in_=planes.rearrange("p j u r -> p r j u"),
                )

        def quantise(u, parts=1, between=None, n=None):
            w_codes[u] = operands.tile([P, H], U32, align_bytes=64, name="w_codes_%d" % u)
            w_scales[u] = operands.tile([P, H], U8, align_bytes=64, name="w_scales_%d" % u)
            width = H // parts
            for part in range(parts):
                cols = slice(part * width, (part + 1) * width)
                nc.vector.quantize_mx(
                    out=w_codes[u][:, cols].bitcast(FP8X4), scales=w_scales[u][:, cols],
                    in_=grouped[u][:, 4 * part * width : 4 * (part + 1) * width],
                )
                if part == 0 and between is not None:
                    between(n)

        acc = {}

        def mx_gate(g, parts=1):
            acc[g] = sums.tile([P, H], F32, name="acc")
            width = H // parts
            for part in range(parts):
                cols = slice(part * width, (part + 1) * width)
                for m in range(2):
                    u = 2 * ORDER.index(g) + m
                    nc.tensor.matmul_mx(
                        out=acc[g][:, cols],
                        lhsT=act_codes[:, m * P : (m + 1) * P].bitcast(FP8X4),
                        lhsT_scale=act_scales[:, m * P : (m + 1) * P],
                        rhs=w_codes[u][:, cols].bitcast(FP8X4),
                        rhs_scale=w_scales[u][:, cols],
                        start=(m == 0),
                        stop=(m == 1),
                    )

        whole = slice(0, H)
        halves = (slice(0, H // 2), slice(H // 2, H))
        stats = {}
        mean_var = {}
        rstd = {}
        centred = {}

        def norm_stats(n, v, parts, first=0, count=None):
            if first == 0:
                stats[n] = kept.tile([P, count or len(parts), 6], F32, name="stats_%d" % n)
            for part, cols in enumerate(parts):
                nc.vector.bn_stats(out=stats[n][:, first + part, :], in_=v[:, cols])

        mean_var_of = {}
        PAIRS = ((I_GATE, G_GATE), (O_GATE, CELL))
        pair_mean_var = {}
        pair_floor = {}
        minus_halves = consts.tile([P, 2], F32)
        nc.gpsimd.memset(minus_halves[:], -0.5)
        for pair in PAIRS:
            pair_mean_var[pair] = kept.tile([P, 2, 2], F32, name="mean_var_%d_%d" % pair)
            for slot, n in enumerate(pair):
                mean_var[n] = pair_mean_var[pair][:, slot, :]

        def pair_norms_floor(pair):
            pair_floor[pair] = kept.tile([P, 2], F32, name="floor_%d_%d" % pair)
            nc.vector.tensor_scalar(
                out=pair_floor[pair][:], in0=pair_mean_var[pair][:, :, 1], scalar1=EPS,
                scalar2=VAR_FLOOR, op0=ALU.is_lt, op1=ALU.mult,
            )

        def pair_norms_rstd(pair):
            pair_padded = kept.tile([P, 2], F32, name="padded_%d_%d" % pair)
            nc.vector.scalar_tensor_tensor(
                out=pair_padded[:], in0=pair_floor[pair][:], scalar=EPS,
                in1=pair_mean_var[pair][:, :, 1], op0=ALU.add, op1=ALU.add,
            )
            pair_rstd = kept.tile([P, 2], F32, name="rstd_%d_%d" % pair)
            nc.gpsimd.tensor_tensor(
                out=pair_rstd[:], in0=pair_padded[:], in1=minus_halves[:], op=ALU.pow
            )
            for slot, n in enumerate(pair):
                rstd[n] = pair_rstd[:, slot : slot + 1]

        def norm_mean(n):
            if n not in mean_var:
                tile = kept.tile([P, 2], F32, name="mean_var_%d" % n)
                mean_var[n] = tile[:]
            nc.vector.bn_aggr(out=mean_var[n], in_=stats[n][:].rearrange("p s k -> p (s k)"))

        passed = {}
        shift = {}
        minus_mean = {}

        def scalar_sum(n, v):
            passed[n] = kept.tile([P, H], F32, name="passed_%d" % n)
            shift[n] = kept.tile([P, 1], F32, name="shift_%d" % n)
            nc.scalar.activation(
                out=passed[n][:], in_=v, func=ACT.Identity, scale=-1.0 / (H * ROOT_H),
                accum_out=shift[n][:],
            )
            minus_mean[n] = kept.tile([P, 1], F32, name="minus_mean_%d" % n)
            nc.gpsimd.tensor_scalar(
                out=minus_mean[n][:], in0=shift[n][:], scalar1=ROOT_H, scalar2=0.0,
                op0=ALU.mult, op1=ALU.add,
            )

        def scalar_var(n):
            nc.scalar.activation(
                out=passed[n][:], in_=passed[n][:], func=ACT.Square, scale=-float(H),
                bias=shift[n][:], accum_out=mean_var[n][:, 1:2],
            )

        def centre_scalar(n, v, cols):
            if n not in centred:
                centred[n] = kept.tile([P, H], F32, name="centred_%d" % n)
            nc.vector.scalar_tensor_tensor(
                out=centred[n][:, cols], in0=v[:, cols], scalar=minus_mean[n][:],
                in1=affine["gamma", n][:, cols], op0=ALU.add, op1=ALU.mult,
            )

        floor = {}

        def norm_floor(n, engine):
            floor[n] = kept.tile([P, 1], F32, name="floor_%d" % n)
            engine.tensor_scalar(
                out=floor[n][:], in0=mean_var[n][:, 1:2], scalar1=EPS, scalar2=VAR_FLOOR,
                op0=ALU.is_lt, op1=ALU.mult,
            )

        padded = {}

        def norm_padded(n, engine):
            padded[n] = kept.tile([P, 1], F32, name="padded_%d" % n)
            engine.tensor_scalar(
                out=padded[n][:], in0=floor[n][:], scalar1=mean_var[n][:, 1:2], scalar2=EPS,
                op0=ALU.add, op1=ALU.add,
            )

        def norm_rstd(n):
            tile = kept.tile([P, 1], F32, name="rstd_%d" % n)
            rstd[n] = tile[:]
            nc.gpsimd.tensor_tensor(
                out=rstd[n], in0=padded[n][:], in1=minus_half[:], op=ALU.pow
            )

        def norm_centre(n, v, cols):
            if n not in centred:
                centred[n] = kept.tile([P, H], F32, name="centred_%d" % n)
            nc.vector.scalar_tensor_tensor(
                out=centred[n][:, cols], in0=v[:, cols], scalar=mean_var[n][:, 0:1],
                in1=affine["gamma", n][:, cols], op0=ALU.subtract, op1=ALU.mult,
            )

        normed = {}

        def norm_finish(n, cols):
            if n not in normed:
                normed[n] = kept.tile([P, H], F32, name="normed_%d" % n)
            nc.vector.scalar_tensor_tensor(
                out=normed[n][:, cols], in0=centred[n][:, cols], scalar=rstd[n],
                in1=affine["beta", n][:, cols], op0=ALU.mult, op1=ALU.add,
            )

        gate = {}

        def apply_function(g, cols):
            if g not in gate:
                gate[g] = kept.tile([P, H], F32, name="gate_%d" % g)
            nc.scalar.activation(
                out=gate[g][:, cols], in_=normed[g][:, cols], func=gate_func[g],
                bias=gate_bias[:, g : g + 1],
            )

        unit_to_k_major(0)
        planes = new_planes()
        transpose_words(planes[:, 0, :, :], x_rows[:].bitcast(F32))
        transpose_words(planes[:, 1, :, :], hx_rows[:].bitcast(F32))
        act_grouped = staging.tile([P, 4 * 2 * P], BF16, align_bytes=64)
        nc.vector.tensor_copy(
            out=act_grouped[:].bitcast(F32).rearrange("p (j r u) -> p j r u", j=2, u=2),
            in_=planes.rearrange("p j u r -> p j r u"),
        )
        quantise(0)
        unit_to_k_major(1)
        act_codes = operands.tile([P, 2 * P], U32, align_bytes=64)
        act_scales = operands.tile([P, 2 * P], U8, align_bytes=64)
        nc.vector.quantize_mx(
            out=act_codes[:].bitcast(FP8X4), scales=act_scales[:], in_=act_grouped[:]
        )
        quantise(1)
        unit_to_k_major(2)
        mx_gate(F_GATE)
        quantise(2)
        norm_stats(F_GATE, acc[F_GATE], (whole,))
        unit_to_k_major(3)
        norm_mean(F_GATE)
        norm_floor(F_GATE, nc.vector)
        quantise(3, 2, lambda n: norm_padded(n, nc.vector), F_GATE)
        norm_rstd(F_GATE)
        for cols in halves:
            norm_centre(F_GATE, acc[F_GATE], cols)
        unit_to_k_major(4)
        unit_to_k_major(5)
        mx_gate(I_GATE)
        quantise(4)
        norm_finish(F_GATE, whole)
        quantise(5, 2)
        mx_gate(G_GATE, 2)
        apply_function(F_GATE, whole)
        held = kept.tile([P, H], F32)
        nc.gpsimd.tensor_tensor(out=held[:], in0=gate[F_GATE][:], in1=cx_rows[:], op=ALU.mult)
        unit_to_k_major(6)
        unit_to_k_major(7)
        norm_stats(I_GATE, acc[I_GATE], (whole,))
        norm_stats(G_GATE, acc[G_GATE], halves[:1], 0, 2)
        norm_mean(I_GATE)
        norm_stats(G_GATE, acc[G_GATE], halves[1:], 1)
        norm_centre(I_GATE, acc[I_GATE], halves[0])
        norm_mean(G_GATE)
        norm_centre(I_GATE, acc[I_GATE], halves[1])
        pair_norms_floor(PAIRS[0])
        norm_centre(G_GATE, acc[G_GATE], halves[0])
        pair_norms_rstd(PAIRS[0])
        norm_centre(G_GATE, acc[G_GATE], halves[1])
        quantise(6)
        norm_finish(I_GATE, whole)
        apply_function(I_GATE, whole)
        for cols in halves:
            norm_finish(G_GATE, cols)
            apply_function(G_GATE, cols)
        quantise(7)
        mx_gate(O_GATE)
        fresh = kept.tile([P, H], F32)
        cell = kept.tile([P, H], F32)
        for cols in halves:
            nc.vector.tensor_tensor(
                out=fresh[:, cols], in0=gate[I_GATE][:, cols], in1=gate[G_GATE][:, cols], op=ALU.mult
            )
        for cols in halves:
            nc.vector.tensor_tensor(
                out=cell[:, cols], in0=held[:, cols], in1=fresh[:, cols], op=ALU.add
            )
        scalar_sum(O_GATE, acc[O_GATE][:])
        scalar_var(O_GATE)
        norm_stats(CELL, cell, halves)
        norm_mean(CELL)
        centre_scalar(O_GATE, acc[O_GATE], halves[0])
        pair_norms_floor(PAIRS[1])
        norm_centre(CELL, cell, halves[0])
        pair_norms_rstd(PAIRS[1])
        centre_scalar(O_GATE, acc[O_GATE], halves[1])
        norm_centre(CELL, cell, halves[1])
        tanh_cy = kept.tile([P, H], F32)
        hy = kept.tile([P, H], F32)
        for cols in halves:
            norm_finish(CELL, cols)
            nc.sync.dma_start(out=out_2[:, cols], in_=normed[CELL][:, cols])
            nc.scalar.activation(out=tanh_cy[:, cols], in_=normed[CELL][:, cols], func=ACT.Tanh)
            norm_finish(O_GATE, cols)
            apply_function(O_GATE, cols)
        for cols in halves:
            nc.vector.tensor_tensor(
                out=hy[:, cols], in0=gate[O_GATE][:, cols], in1=tanh_cy[:, cols], op=ALU.mult
            )
            nc.sync.dma_start(out=out_0[:, cols], in_=hy[:, cols])
            nc.sync.dma_start(out=out_1[:, cols], in_=hy[:, cols])
